import numpy as np
import ml_dtypes


def mxq(x, axis, fmt="e4m3"):
    dtype, down = {"e4m3": (ml_dtypes.float8_e4m3fn, 7), "e5m2": (ml_dtypes.float8_e5m2, 14)}[fmt]
    v = np.moveaxis(np.asarray(x, np.float32).astype(ml_dtypes.bfloat16).astype(np.float64), axis, -1)
    blocks = v.reshape(v.shape[:-1] + (-1, 32))
    amax = np.abs(blocks).max(-1, keepdims=True)
    byte = np.maximum(np.where(amax > 0, np.frexp(amax)[1] - 1 + 127, 0) - down, 1)
    scale = np.exp2(byte - 127.0)
    codes = (blocks / scale).astype(np.float32).astype(dtype).astype(np.float64)
    return np.moveaxis((codes * scale).reshape(v.shape), -1, axis)


WIDE = False


def mx_kscale(k):
    if not WIDE:
        return np.ones(k)
    levels = np.array([10, -10, 5, -5, 0])
    a = np.random.permutation(np.resize(levels, k // 512 * 4)).reshape(k // 512, 4)
    idx = np.arange(k)
    return np.exp2(a[idx // 512, idx % 128 // 32])


BF16 = ml_dtypes.bfloat16


def bf(x):
    return np.asarray(x, np.float32).astype(BF16)


def f64(x):
    return np.asarray(x).astype(np.float64)


E2M1 = np.array([0.0, 0.5, 1.0, 1.5, 2.0, 3.0, 4.0, 6.0, -0.0, -0.5, -1.0, -1.5, -2.0, -3.0, -4.0, -6.0])


def pack_weight(w, fmt):
    k, n = w.shape
    w = f64(bf(w)).reshape(k // 32, 32, n)
    amax = np.abs(w).max(1)
    if fmt == "e4m3":
        byte = np.frexp(amax)[1] - 1 + 127 - 7
    else:
        mant, ex = np.frexp(amax / 6.0)
        byte = np.where(mant > 0.5, ex, ex - 1) + 127
    byte = np.clip(np.where(amax > 0, byte, 1), 1, 254)
    scaled = (w * np.exp2(127.0 - byte)[:, None, :]).reshape(k, n).astype(np.float32)
    by_word = np.ascontiguousarray(scaled.reshape(k // 512, 128, 4, n).transpose(0, 1, 3, 2))
    if fmt == "e4m3":
        words = by_word.astype(ml_dtypes.float8_e4m3fn).view(np.uint8)
    else:
        c = by_word.astype(ml_dtypes.float4_e2m1fn).view(np.uint8) & 0xF
        words = c[..., 0::2] | (c[..., 1::2] << 4)
    return np.ascontiguousarray(words), np.ascontiguousarray(byte.astype(np.uint8).reshape(k // 512, 16, n))


def unpack_weight(words, scales, fmt):
    g, p, n, _ = words.shape
    if fmt == "e4m3":
        vals = np.ascontiguousarray(words).view(ml_dtypes.float8_e4m3fn).astype(np.float64)
    else:
        nib = np.empty((g, p, n, 4), np.uint8)
        nib[..., 0::2] = words & 0xF
        nib[..., 1::2] = words >> 4
        vals = E2M1[nib]
    vals = vals * np.repeat(np.exp2(scales.astype(np.float64) - 127.0), 8, axis=1)[..., None]
    return vals.transpose(0, 1, 3, 2).reshape(g * 512, n)


B, DH, DO, L = 1024, 2048, 1024, 128


def setup_inputs():
    s = mx_kscale(2 * DH)
    t = mx_kscale(DO)
    sbj_vec = bf(np.random.standard_normal((B, DH)) * s[:DH])
    obj_vec = bf(np.random.standard_normal((B, DH)) * s[DH:])
    W1_words, W1_scales = pack_weight(np.random.standard_normal((2 * DH, DO)) * 1.28 / np.sqrt(2 * DH) / s[:, None] * t, "e4m3")
    b1 = bf(np.random.standard_normal(DO) * 0.1 * t)
    W2_words, W2_scales = pack_weight(np.random.standard_normal((DO, DO)) * 12.0 / DO / t[:, None], "e4m3")
    b2 = bf(np.random.standard_normal(DO) * 0.1)
    label_vecs = bf(np.random.standard_normal((L, DO)) * 8.0 / np.sqrt(DO))
    return {"sbj_vec": sbj_vec,
            "obj_vec": obj_vec,
            "W1_words": W1_words,
            "W1_scales": W1_scales,
            "b1": b1,
            "W2_words": W2_words,
            "W2_scales": W2_scales,
            "b2": b2,
            "label_vecs": label_vecs}


def reference(sbj_vec, obj_vec, W1_words, W1_scales, b1, W2_words, W2_scales, b2, label_vecs):
    x = np.concatenate([f64(sbj_vec), f64(obj_vec)], axis=1)
    hidden = (mxq(np.maximum(x, 0.0), 1, "e4m3") @ unpack_weight(W1_words, W1_scales, "e4m3")) + f64(b1)
    emb = (mxq(np.maximum(hidden, 0.0), 1, "e4m3") @ unpack_weight(W2_words, W2_scales, "e4m3")) + f64(b2)
    lab = f64(label_vecs)
    scores = np.empty((emb.shape[0], lab.shape[0]))
    for l in range(lab.shape[0]):
        diff = np.maximum(lab[l][None, :] - emb, 0.0)
        scores[:, l] = -np.sqrt(np.sum(diff * diff, axis=1))
    return scores

@@ -1,0 +1,285 @@
+from contextlib import ExitStack
+
+import concourse.mybir as mybir
+from concourse.masks import make_identity
+
+F32 = mybir.dt.float32
+BF16 = mybir.dt.bfloat16
+I32 = mybir.dt.int32
+U32 = mybir.dt.uint32
+U8 = mybir.dt.uint8
+FP8X4 = mybir.dt.float8_e4m3fn_x4
+ALU = mybir.AluOpType
+ACT = mybir.ActivationFunctionType
+
+P = 128
+B = 1024
+DH = 2048
+K1 = 2 * DH
+DO = 1024
+L = 128
+
+PACK = 4
+K_PASS = P * PACK
+WORDS_PASS = K_PASS // 2
+N_MOVING = 512
+B_TILES = B // P
+D_CHUNKS = DO // P
+TURNS_PER_BANK = 4
+PLANES_PER_TILE = 4
+
+FLOPS = 2 * B * K1 * DO + 2 * B * DO * DO + 4 * B * L * DO
+
+
+def load_quantised_weight(nc, pool, words, scales, name):
+    passes, width = words.shape[0], words.shape[2]
+    together = min(passes, PLANES_PER_TILE)
+    codes = pool.tile([P, passes, width], U32, name=name + "_codes", align_bytes=64)
+    planes = pool.tile([P, passes // together, width], U8, name=name + "_planes", align_bytes=64)
+    nc.vector.memset(planes[:].bitcast(I32), 0)
+    for group in range(passes // together):
+        for quadrant in range(4):
+            nc.sync.dma_start(
+                out=planes[32 * quadrant : 32 * quadrant + 4 * together, group, :].bitcast(I32),
+                in_=scales[
+                    group * together : (group + 1) * together, 4 * quadrant : 4 * quadrant + 4, :
+                ].bitcast(I32),
+            )
+    for g in range(passes):
+        nc.sync.dma_start(
+            out=codes[:, g, :].bitcast(I32),
+            in_=words[g].rearrange("p n t -> p (n t)").bitcast(I32),
+        )
+    return codes, planes
+
+
+def scale_plane(planes, g, cols):
+    return planes[4 * (g % PLANES_PER_TILE) : P, g // PLANES_PER_TILE, cols]
+
+
+def turn_k_onto_partitions(nc, psum, ident, rows, grouped_words, scalar_helps):
+    words = rows.bitcast(F32)
+    for pair in range(words.shape[1] // (2 * WORDS_PASS)):
+        bank = psum.tile([P, TURNS_PER_BANK, P], F32, name="turned")
+        for j in range(TURNS_PER_BANK):
+            g, u = 2 * pair + j // 2, j % 2
+            nc.tensor.transpose(
+                bank[:, j, :], words[:, WORDS_PASS * g + u : WORDS_PASS * (g + 1) : 2], ident
+            )
+        copy = nc.scalar.copy if (scalar_helps and pair % 2 == 1) else nc.vector.tensor_copy
+        copy(
+            out=grouped_words[:, 2 * pair : 2 * pair + 2, :, :],
+            in_=bank[:].rearrange("p (g u) r -> p g r u", u=2),
+        )
+
+
+def embed(tc, ident, emb_t, lab_t, sbj_vec, obj_vec, W1_words, W1_scales, b1, W2_words, W2_scales, b2, label_vecs):
+    nc = tc.nc
+    with ExitStack() as ctx:
+        fixed = ctx.enter_context(tc.tile_pool(name="fixed", bufs=1))
+        stream = ctx.enter_context(tc.tile_pool(name="stream", bufs=2))
+        loads = ctx.enter_context(tc.tile_pool(name="loads", bufs=3))
+        turned = ctx.enter_context(tc.psum_pool(name="turned", bufs=3))
+        sums = ctx.enter_context(tc.psum_pool(name="sums", bufs=4))
+
+        w1_codes, w1_planes = load_quantised_weight(nc, fixed, W1_words, W1_scales, "w1")
+        w2_codes, w2_planes = load_quantised_weight(nc, fixed, W2_words, W2_scales, "w2")
+
+        b1_all = fixed.tile([P, DO], BF16)
+        nc.scalar.dma_start(out=b1_all[:], in_=b1.partition_broadcast(P))
+
+        lab_rows = fixed.tile([P, DO], BF16)
+        nc.scalar.dma_start(out=lab_rows[:], in_=label_vecs)
+        lab_f32 = fixed.tile([P, DO], F32)
+        nc.vector.tensor_copy(out=lab_f32[:], in_=lab_rows[:])
+        for half in range(D_CHUNKS // TURNS_PER_BANK):
+            bank = turned.tile([P, TURNS_PER_BANK, P], F32, name="turned")
+            for j in range(TURNS_PER_BANK):
+                c = half * TURNS_PER_BANK + j
+                nc.tensor.transpose(bank[:, j, :], lab_f32[:, c * P : (c + 1) * P], ident)
+            nc.vector.tensor_copy(
+                out=lab_t[:, half * TURNS_PER_BANK : (half + 1) * TURNS_PER_BANK, :], in_=bank[:]
+            )
+
+        b2_rows = fixed.tile([P, P], BF16)
+        nc.vector.memset(b2_rows[:], 0.0)
+        nc.scalar.dma_start(out=b2_rows[0:D_CHUNKS, :], in_=b2.rearrange("(c p) -> c p", p=P))
+        b2_f32 = fixed.tile([P, P], F32)
+        nc.vector.tensor_copy(out=b2_f32[:], in_=b2_rows[:])
+        b2_bank = turned.tile([P, TURNS_PER_BANK, P], F32, name="turned")
+        nc.tensor.transpose(b2_bank[:, 0, :], b2_f32[:], ident)
+        b2_t = fixed.tile([P, D_CHUNKS], F32)
+        nc.vector.tensor_copy(out=b2_t[:], in_=b2_bank[:, 0, 0:D_CHUNKS])
+
+        h_grouped = fixed.tile([P, DO // K_PASS, B, PACK], BF16, align_bytes=64)
+        h_codes = fixed.tile([P, DO // K_PASS, B], U32, align_bytes=64)
+        h_scales = fixed.tile([P, DO // K_PASS, B], U8, align_bytes=64)
+
+        for i in range(B_TILES):
+            b_rows = slice(i * P, (i + 1) * P)
+            x_rows = loads.tile([P, K1], BF16)
+            nc.scalar.dma_start(out=x_rows[:, 0:DH], in_=sbj_vec[b_rows, :])
+            nc.scalar.dma_start(out=x_rows[:, DH:K1], in_=obj_vec[b_rows, :])
+            nc.vector.tensor_scalar_max(out=x_rows[:], in0=x_rows[:], scalar1=0.0)
+
+            x_grouped = stream.tile([P, K1 // K_PASS, P, PACK], BF16, align_bytes=64)
+            turn_k_onto_partitions(nc, turned, ident, x_rows[:], x_grouped[:].bitcast(F32), True)
+            x_codes = stream.tile([P, K1 // K_PASS, P], U32, align_bytes=64)
+            x_scales = stream.tile([P, K1 // K_PASS, P], U8, align_bytes=64)
+            nc.vector.quantize_mx(
+                out=x_codes[:].rearrange("p g r -> p (g r)").bitcast(FP8X4),
+                scales=x_scales[:].rearrange("p g r -> p (g r)"),
+                in_=x_grouped[:].rearrange("p g r t -> p (g r t)"),
+            )
+
+            h_rows = stream.tile([P, DO], BF16)
+            for n in range(DO // N_MOVING):
+                n_cols = slice(n * N_MOVING, (n + 1) * N_MOVING)
+                acc = sums.tile([P, N_MOVING], F32, name="acc")
+                for g in range(K1 // K_PASS):
+                    nc.tensor.matmul_mx(
+                        out=acc[:],
+                        lhsT=x_codes[:, g, :].bitcast(FP8X4),
+                        lhsT_scale=x_scales[:, g, :],
+                        rhs=w1_codes[:, g, n_cols].bitcast(FP8X4),
+                        rhs_scale=scale_plane(w1_planes, g, n_cols),
+                        start=(g == 0),
+                        stop=(g == K1 // K_PASS - 1),
+                    )
+                hidden = stream.tile([P, N_MOVING], F32)
+                nc.vector.tensor_tensor(out=hidden[:], in0=acc[:], in1=b1_all[:, n_cols], op=ALU.add)
+                nc.scalar.activation(out=h_rows[:, n_cols], in_=hidden[:], func=ACT.Relu)
+            turn_k_onto_partitions(
+                nc, turned, ident, h_rows[:], h_grouped[:, :, b_rows, :].bitcast(F32), False
+            )
+
+        for n in range(B // N_MOVING):
+            b_cols = slice(n * N_MOVING, (n + 1) * N_MOVING)
+            for g in range(DO // K_PASS):
+                nc.vector.quantize_mx(
+                    out=h_codes[:, g, b_cols].bitcast(FP8X4),
+                    scales=h_scales[:, g, b_cols],
+                    in_=h_grouped[:, g, b_cols, :].rearrange("p r t -> p (r t)"),
+                )
+            for c in range(D_CHUNKS):
+                d_cols = slice(c * P, (c + 1) * P)
+                acc = sums.tile([P, N_MOVING], F32, name="acc")
+                for g in range(DO // K_PASS):
+                    nc.tensor.matmul_mx(
+                        out=acc[:],
+                        lhsT=w2_codes[:, g, d_cols].bitcast(FP8X4),
+                        lhsT_scale=scale_plane(w2_planes, g, d_cols),
+                        rhs=h_codes[:, g, b_cols].bitcast(FP8X4),
+                        rhs_scale=h_scales[:, g, b_cols],
+                        start=(g == 0),
+                        stop=(g == DO // K_PASS - 1),
+                    )
+                nc.scalar.activation(
+                    out=emb_t[:, c, b_cols], in_=acc[:], func=ACT.Identity, bias=b2_t[:, c : c + 1]
+                )
+
+
+HALF_CHUNKS = TURNS_PER_BANK
+HALVES = D_CHUNKS // HALF_CHUNKS
+QUARTET = 4
+QUARTETS = B_TILES // QUARTET
+STATS = 6
+SQRT_FLOOR = 1e-30
+
+
+def label_distances(tc, ident, emb_t, lab_t, out):
+    nc = tc.nc
+    with ExitStack() as ctx:
+        fixed = ctx.enter_context(tc.tile_pool(name="results", bufs=1))
+        diffs = ctx.enter_context(tc.tile_pool(name="diffs", bufs=3))
+        waste = ctx.enter_context(tc.tile_pool(name="waste", bufs=2))
+        banks = ctx.enter_context(tc.psum_pool(name="banks", bufs=8))
+
+        by_scalar = fixed.tile([P, HALVES, QUARTETS, QUARTET - 1, L], F32)
+        by_vector = fixed.tile([P, QUARTETS, L, HALVES, STATS], F32)
+
+        def clip_differences(diff, step, chunks):
+            label, half = step
+            for j in chunks:
+                c = half * HALF_CHUNKS + j
+                nc.vector.tensor_scalar(
+                    out=diff[:, j, :],
+                    in0=emb_t[:, c, :],
+                    scalar1=lab_t[:, c, label : label + 1],
+                    scalar2=0.0,
+                    op0=ALU.subtract,
+                    op1=ALU.min,
+                )
+
+        steps = [(label, half) for label in range(L) for half in range(HALVES)]
+        per_quartet = HALF_CHUNKS // QUARTETS
+        with tc.manual_schedule():
+            diff = diffs.tile([P, HALF_CHUNKS, B], F32, name="diff")
+            clip_differences(diff, steps[0], range(HALF_CHUNKS))
+            for s, (label, half) in enumerate(steps):
+                following = steps[s + 1] if s + 1 < len(steps) else None
+                if following is not None:
+                    diff_next = diffs.tile([P, HALF_CHUNKS, B], F32, name="diff")
+                for quartet in range(QUARTETS):
+                    if following is not None:
+                        clip_differences(
+                            diff_next, following, range(quartet * per_quartet, (quartet + 1) * per_quartet)
+                        )
+                    for place in range(QUARTET):
+                        b_cols = slice((quartet * QUARTET + place) * P, (quartet * QUARTET + place + 1) * P)
+                        bank = banks.tile([P, HALF_CHUNKS, P], F32, name="bank")
+                        for j in range(HALF_CHUNKS):
+                            nc.tensor.transpose(bank[:, j, :], diff[:, j, b_cols], ident)
+                        if place < QUARTET - 1:
+                            squares = waste.tile([P, HALF_CHUNKS, P], F32, name="squares")
+                            nc.scalar.activation(
+                                out=squares[:],
+                                in_=bank[:],
+                                func=ACT.Square,
+                                accum_out=by_scalar[:, half, quartet, place, label : label + 1],
+                            )
+                        else:
+                            nc.vector.bn_stats(out=by_vector[:, quartet, label, half, :], in_=bank[:])
+                if following is not None:
+                    diff = diff_next
+
+        total = fixed.tile([P, QUARTETS, QUARTET, L], F32)
+        nc.vector.tensor_tensor(
+            out=total[:, :, 0 : QUARTET - 1, :], in0=by_scalar[:, 0, :, :, :], in1=by_scalar[:, 1, :, :, :], op=ALU.add
+        )
+        stats = by_vector[:].rearrange("p q l h (e s) -> p (q l) (h e) s", s=3)
+        parts = fixed.tile([P, QUARTETS * L, 2 * HALVES], F32)
+        count = float(HALF_CHUNKS * P // 2)
+        nc.vector.tensor_tensor(out=parts[:], in0=stats[:, :, :, 1], in1=stats[:, :, :, 1], op=ALU.mult)
+        nc.vector.tensor_scalar_mul(out=parts[:], in0=parts[:], scalar1=count)
+        nc.vector.tensor_tensor(out=parts[:], in0=parts[:], in1=stats[:, :, :, 2], op=ALU.add)
+        nc.vector.tensor_reduce(
+            out=total[:, :, QUARTET - 1, :],
+            in_=parts[:].rearrange("p (q l) s -> p q l s", q=QUARTETS),
+            axis=mybir.AxisListType.X,
+            op=ALU.add,
+        )
+
+        nc.vector.tensor_scalar_max(out=total[:], in0=total[:], scalar1=SQRT_FLOOR)
+        scores = fixed.tile([P, QUARTETS, QUARTET, L], F32)
+        nc.scalar.activation(out=scores[:], in_=total[:], func=ACT.Sqrt)
+        nc.vector.tensor_scalar_mul(out=scores[:], in0=scores[:], scalar1=-1.0)
+        nc.sync.dma_start(
+            out=out.rearrange("(t p) l -> p t l", p=P), in_=scores[:].rearrange("p q i l -> p (q i) l")
+        )
+
+
+def tile_relationembedding_kernel(
+    tc, sbj_vec, obj_vec, W1_words, W1_scales, b1, W2_words, W2_scales, b2, label_vecs, out
+):
+    nc = tc.nc
+    with tc.tile_pool(name="keep", bufs=1) as keep:
+        ident = keep.tile([P, P], F32)
+        make_identity(nc, ident[:])
+        emb_t = keep.tile([P, D_CHUNKS, B], F32)
+        lab_t = keep.tile([P, D_CHUNKS, L], F32)
+        embed(
+            tc, ident[:], emb_t, lab_t,
+            sbj_vec, obj_vec, W1_words, W1_scales, b1, W2_words, W2_scales, b2, label_vecs,
+        )
+        label_distances(tc, ident[:], emb_t, lab_t, out)

@@ -73,98 +73,125 @@ def turn_k_onto_partitions(nc, psum, ident, rows, grouped_words, scalar_helps):
         )
 
 
+AHEAD = 2
+
+
 def embed(tc, ident, emb_t, lab_t, sbj_vec, obj_vec, W1_words, W1_scales, b1, W2_words, W2_scales, b2, label_vecs):
     nc = tc.nc
+    passes_1, passes_2 = K1 // K_PASS, DO // K_PASS
     with ExitStack() as ctx:
         fixed = ctx.enter_context(tc.tile_pool(name="fixed", bufs=1))
-        stream = ctx.enter_context(tc.tile_pool(name="stream", bufs=2))
-        loads = ctx.enter_context(tc.tile_pool(name="loads", bufs=3))
-        turned = ctx.enter_context(tc.psum_pool(name="turned", bufs=3))
+        double = ctx.enter_context(tc.tile_pool(name="double", bufs=2))
+        triple = ctx.enter_context(tc.tile_pool(name="triple", bufs=AHEAD + 1))
+        turned = ctx.enter_context(tc.psum_pool(name="turned", bufs=4))
         sums = ctx.enter_context(tc.psum_pool(name="sums", bufs=4))
 
-        w1_codes, w1_planes = load_quantised_weight(nc, fixed, W1_words, W1_scales, "w1")
-        w2_codes, w2_planes = load_quantised_weight(nc, fixed, W2_words, W2_scales, "w2")
+        x_rows = [fixed.tile([P, K1], BF16, name="x_rows_%d" % i) for i in range(B_TILES)]
+
+        def load_x(i):
+            b_rows = slice(i * P, (i + 1) * P)
+            nc.sync.dma_start(out=x_rows[i][:, 0:DH], in_=sbj_vec[b_rows, :])
+            nc.sync.dma_start(out=x_rows[i][:, DH:K1], in_=obj_vec[b_rows, :])
 
         b1_all = fixed.tile([P, DO], BF16)
         nc.scalar.dma_start(out=b1_all[:], in_=b1.partition_broadcast(P))
-
+        for i in range(AHEAD):
+            load_x(i)
         lab_rows = fixed.tile([P, DO], BF16)
-        nc.scalar.dma_start(out=lab_rows[:], in_=label_vecs)
-        lab_f32 = fixed.tile([P, DO], F32)
-        nc.vector.tensor_copy(out=lab_f32[:], in_=lab_rows[:])
-        for half in range(D_CHUNKS // TURNS_PER_BANK):
-            bank = turned.tile([P, TURNS_PER_BANK, P], F32, name="turned")
-            for j in range(TURNS_PER_BANK):
-                c = half * TURNS_PER_BANK + j
-                nc.tensor.transpose(bank[:, j, :], lab_f32[:, c * P : (c + 1) * P], ident)
-            nc.vector.tensor_copy(
-                out=lab_t[:, half * TURNS_PER_BANK : (half + 1) * TURNS_PER_BANK, :], in_=bank[:]
-            )
-
+        nc.sync.dma_start(out=lab_rows[:], in_=label_vecs)
         b2_rows = fixed.tile([P, P], BF16)
         nc.vector.memset(b2_rows[:], 0.0)
-        nc.scalar.dma_start(out=b2_rows[0:D_CHUNKS, :], in_=b2.rearrange("(c p) -> c p", p=P))
-        b2_f32 = fixed.tile([P, P], F32)
-        nc.vector.tensor_copy(out=b2_f32[:], in_=b2_rows[:])
-        b2_bank = turned.tile([P, TURNS_PER_BANK, P], F32, name="turned")
-        nc.tensor.transpose(b2_bank[:, 0, :], b2_f32[:], ident)
-        b2_t = fixed.tile([P, D_CHUNKS], F32)
-        nc.vector.tensor_copy(out=b2_t[:], in_=b2_bank[:, 0, 0:D_CHUNKS])
+        nc.sync.dma_start(out=b2_rows[0:D_CHUNKS, :], in_=b2.rearrange("(c p) -> c p", p=P))
+        w1_codes, w1_planes = load_quantised_weight(nc, fixed, W1_words, W1_scales, "w1")
+        for i in range(AHEAD, B_TILES):
+            load_x(i)
+        w2_codes, w2_planes = load_quantised_weight(nc, fixed, W2_words, W2_scales, "w2")
 
-        h_grouped = fixed.tile([P, DO // K_PASS, B, PACK], BF16, align_bytes=64)
-        h_codes = fixed.tile([P, DO // K_PASS, B], U32, align_bytes=64)
-        h_scales = fixed.tile([P, DO // K_PASS, B], U8, align_bytes=64)
+        x_codes, x_scales, x_grouped = {}, {}, {}
 
-        for i in range(B_TILES):
-            b_rows = slice(i * P, (i + 1) * P)
-            x_rows = loads.tile([P, K1], BF16)
-            nc.scalar.dma_start(out=x_rows[:, 0:DH], in_=sbj_vec[b_rows, :])
-            nc.scalar.dma_start(out=x_rows[:, DH:K1], in_=obj_vec[b_rows, :])
-            nc.vector.tensor_scalar_max(out=x_rows[:], in0=x_rows[:], scalar1=0.0)
+        def relu_x(i):
+            nc.vector.tensor_scalar_max(out=x_rows[i][:], in0=x_rows[i][:], scalar1=0.0)
 
-            x_grouped = stream.tile([P, K1 // K_PASS, P, PACK], BF16, align_bytes=64)
-            turn_k_onto_partitions(nc, turned, ident, x_rows[:], x_grouped[:].bitcast(F32), True)
-            x_codes = stream.tile([P, K1 // K_PASS, P], U32, align_bytes=64)
-            x_scales = stream.tile([P, K1 // K_PASS, P], U8, align_bytes=64)
+        def turn_x(i):
+            x_grouped[i] = double.tile([P, passes_1, P, PACK], BF16, name="x_grouped", align_bytes=64)
+            turn_k_onto_partitions(nc, turned, ident, x_rows[i][:], x_grouped[i][:].bitcast(F32), True)
+
+        def quantise_x(i):
+            x_codes[i] = triple.tile([P, passes_1, P], U32, name="x_codes", align_bytes=64)
+            x_scales[i] = triple.tile([P, passes_1, P], U8, name="x_scales", align_bytes=64)
             nc.vector.quantize_mx(
-                out=x_codes[:].rearrange("p g r -> p (g r)").bitcast(FP8X4),
-                scales=x_scales[:].rearrange("p g r -> p (g r)"),
-                in_=x_grouped[:].rearrange("p g r t -> p (g r t)"),
+                out=x_codes[i][:].rearrange("p g r -> p (g r)").bitcast(FP8X4),
+                scales=x_scales[i][:].rearrange("p g r -> p (g r)"),
+                in_=x_grouped[i][:].rearrange("p g r t -> p (g r t)"),
             )
 
-            h_rows = stream.tile([P, DO], BF16)
-            for n in range(DO // N_MOVING):
-                n_cols = slice(n * N_MOVING, (n + 1) * N_MOVING)
-                acc = sums.tile([P, N_MOVING], F32, name="acc")
-                for g in range(K1 // K_PASS):
+        b2_t = fixed.tile([P, D_CHUNKS], F32)
+
+        def turn_labels_and_b2():
+            lab_f32 = fixed.tile([P, DO], F32)
+            nc.vector.tensor_copy(out=lab_f32[:], in_=lab_rows[:])
+            b2_f32 = fixed.tile([P, P], F32)
+            nc.vector.tensor_copy(out=b2_f32[:], in_=b2_rows[:])
+            for half in range(D_CHUNKS // TURNS_PER_BANK):
+                bank = turned.tile([P, TURNS_PER_BANK, P], F32, name="turned")
+                for j in range(TURNS_PER_BANK):
+                    c = half * TURNS_PER_BANK + j
+                    nc.tensor.transpose(bank[:, j, :], lab_f32[:, c * P : (c + 1) * P], ident)
+                nc.vector.tensor_copy(
+                    out=lab_t[:, half * TURNS_PER_BANK : (half + 1) * TURNS_PER_BANK, :], in_=bank[:]
+                )
+            bank = turned.tile([P, TURNS_PER_BANK, P], F32, name="turned")
+            nc.tensor.transpose(bank[:, 0, :], b2_f32[:], ident)
+            nc.vector.tensor_copy(out=b2_t[:], in_=bank[:, 0, 0:D_CHUNKS])
+
+        h_rows = {}
+        h_grouped = fixed.tile([P, passes_2, B, PACK], BF16, align_bytes=64)
+        h_codes = fixed.tile([P, passes_2, B], U32, align_bytes=64)
+        h_scales = fixed.tile([P, passes_2, B], U8, align_bytes=64)
+
+        def first_layer(i):
+            halves = range(DO // N_MOVING)
+            acc = [sums.tile([P, N_MOVING], F32, name="acc") for n in halves]
+            for g in range(passes_1):
+                for n in halves:
+                    n_cols = slice(n * N_MOVING, (n + 1) * N_MOVING)
                     nc.tensor.matmul_mx(
-                        out=acc[:],
-                        lhsT=x_codes[:, g, :].bitcast(FP8X4),
-                        lhsT_scale=x_scales[:, g, :],
+                        out=acc[n][:],
+                        lhsT=x_codes[i][:, g, :].bitcast(FP8X4),
+                        lhsT_scale=x_scales[i][:, g, :],
                         rhs=w1_codes[:, g, n_cols].bitcast(FP8X4),
                         rhs_scale=scale_plane(w1_planes, g, n_cols),
                         start=(g == 0),
-                        stop=(g == K1 // K_PASS - 1),
+                        stop=(g == passes_1 - 1),
                     )
-                hidden = stream.tile([P, N_MOVING], F32)
-                nc.vector.tensor_tensor(out=hidden[:], in0=acc[:], in1=b1_all[:, n_cols], op=ALU.add)
-                nc.scalar.activation(out=h_rows[:, n_cols], in_=hidden[:], func=ACT.Relu)
+            h_rows[i] = double.tile([P, DO], BF16, name="h_rows")
+            for n in halves:
+                n_cols = slice(n * N_MOVING, (n + 1) * N_MOVING)
+                hidden = double.tile([P, N_MOVING], F32, name="hidden")
+                nc.vector.tensor_tensor(out=hidden[:], in0=acc[n][:], in1=b1_all[:, n_cols], op=ALU.add)
+                nc.scalar.activation(out=h_rows[i][:, n_cols], in_=hidden[:], func=ACT.Relu)
+
+        def turn_hidden(i):
+            b_rows = slice(i * P, (i + 1) * P)
             turn_k_onto_partitions(
-                nc, turned, ident, h_rows[:], h_grouped[:, :, b_rows, :].bitcast(F32), False
+                nc, turned, ident, h_rows[i][:], h_grouped[:, :, b_rows, :].bitcast(F32), False
             )
 
-        for n in range(B // N_MOVING):
+        def quantise_hidden(n):
             b_cols = slice(n * N_MOVING, (n + 1) * N_MOVING)
-            for g in range(DO // K_PASS):
+            for g in range(passes_2):
                 nc.vector.quantize_mx(
                     out=h_codes[:, g, b_cols].bitcast(FP8X4),
                     scales=h_scales[:, g, b_cols],
                     in_=h_grouped[:, g, b_cols, :].rearrange("p r t -> p (r t)"),
                 )
-            for c in range(D_CHUNKS):
+
+        def second_layer(n, chunks):
+            b_cols = slice(n * N_MOVING, (n + 1) * N_MOVING)
+            for c in chunks:
                 d_cols = slice(c * P, (c + 1) * P)
                 acc = sums.tile([P, N_MOVING], F32, name="acc")
-                for g in range(DO // K_PASS):
+                for g in range(passes_2):
                     nc.tensor.matmul_mx(
                         out=acc[:],
                         lhsT=w2_codes[:, g, d_cols].bitcast(FP8X4),
@@ -172,11 +199,35 @@ def embed(tc, ident, emb_t, lab_t, sbj_vec, obj_vec, W1_words, W1_scales, b1, W2
                         rhs=h_codes[:, g, b_cols].bitcast(FP8X4),
                         rhs_scale=h_scales[:, g, b_cols],
                         start=(g == 0),
-                        stop=(g == DO // K_PASS - 1),
+                        stop=(g == passes_2 - 1),
                     )
                 nc.scalar.activation(
                     out=emb_t[:, c, b_cols], in_=acc[:], func=ACT.Identity, bias=b2_t[:, c : c + 1]
                 )
+
+        for i in range(AHEAD):
+            relu_x(i)
+            turn_x(i)
+        quantise_x(0)
+        turn_labels_and_b2()
+        for i in range(1, AHEAD):
+            quantise_x(i)
+        for i in range(B_TILES):
+            later = i + AHEAD
+            if later < B_TILES:
+                relu_x(later)
+            first_layer(i)
+            if later < B_TILES:
+                turn_x(later)
+            else:
+                share = D_CHUNKS // AHEAD
+                second_layer(0, range((later - B_TILES) * share, (later - B_TILES + 1) * share))
+            turn_hidden(i)
+            if later < B_TILES:
+                quantise_x(later)
+            if (i + 1) * P % N_MOVING == 0:
+                quantise_hidden(i * P // N_MOVING)
+        second_layer(1, range(D_CHUNKS))
 
 
 HALF_CHUNKS = TURNS_PER_BANK
@@ -213,35 +264,34 @@ def label_distances(tc, ident, emb_t, lab_t, out):
 
         steps = [(label, half) for label in range(L) for half in range(HALVES)]
         per_quartet = HALF_CHUNKS // QUARTETS
-        with tc.manual_schedule():
-            diff = diffs.tile([P, HALF_CHUNKS, B], F32, name="diff")
-            clip_differences(diff, steps[0], range(HALF_CHUNKS))
-            for s, (label, half) in enumerate(steps):
-                following = steps[s + 1] if s + 1 < len(steps) else None
+        diff = diffs.tile([P, HALF_CHUNKS, B], F32, name="diff")
+        clip_differences(diff, steps[0], range(HALF_CHUNKS))
+        for s, (label, half) in enumerate(steps):
+            following = steps[s + 1] if s + 1 < len(steps) else None
+            if following is not None:
+                diff_next = diffs.tile([P, HALF_CHUNKS, B], F32, name="diff")
+            for quartet in range(QUARTETS):
                 if following is not None:
-                    diff_next = diffs.tile([P, HALF_CHUNKS, B], F32, name="diff")
-                for quartet in range(QUARTETS):
-                    if following is not None:
-                        clip_differences(
-                            diff_next, following, range(quartet * per_quartet, (quartet + 1) * per_quartet)
+                    clip_differences(
+                        diff_next, following, range(quartet * per_quartet, (quartet + 1) * per_quartet)
+                    )
+                for place in range(QUARTET):
+                    b_cols = slice((quartet * QUARTET + place) * P, (quartet * QUARTET + place + 1) * P)
+                    bank = banks.tile([P, HALF_CHUNKS, P], F32, name="bank")
+                    for j in range(HALF_CHUNKS):
+                        nc.tensor.transpose(bank[:, j, :], diff[:, j, b_cols], ident)
+                    if place < QUARTET - 1:
+                        squares = waste.tile([P, HALF_CHUNKS, P], F32, name="squares")
+                        nc.scalar.activation(
+                            out=squares[:],
+                            in_=bank[:],
+                            func=ACT.Square,
+                            accum_out=by_scalar[:, half, quartet, place, label : label + 1],
                         )
-                    for place in range(QUARTET):
-                        b_cols = slice((quartet * QUARTET + place) * P, (quartet * QUARTET + place + 1) * P)
-                        bank = banks.tile([P, HALF_CHUNKS, P], F32, name="bank")
-                        for j in range(HALF_CHUNKS):
-                            nc.tensor.transpose(bank[:, j, :], diff[:, j, b_cols], ident)
-                        if place < QUARTET - 1:
-                            squares = waste.tile([P, HALF_CHUNKS, P], F32, name="squares")
-                            nc.scalar.activation(
-                                out=squares[:],
-                                in_=bank[:],
-                                func=ACT.Square,
-                                accum_out=by_scalar[:, half, quartet, place, label : label + 1],
-                            )
-                        else:
-                            nc.vector.bn_stats(out=by_vector[:, quartet, label, half, :], in_=bank[:])
-                if following is not None:
-                    diff = diff_next
+                    else:
+                        nc.vector.bn_stats(out=by_vector[:, quartet, label, half, :], in_=bank[:])
+            if following is not None:
+                diff = diff_next
 
         total = fixed.tile([P, QUARTETS, QUARTET, L], F32)
         nc.vector.tensor_tensor(
@@ -273,7 +323,7 @@ def tile_relationembedding_kernel(
     tc, sbj_vec, obj_vec, W1_words, W1_scales, b1, W2_words, W2_scales, b2, label_vecs, out
 ):
     nc = tc.nc
-    with tc.tile_pool(name="keep", bufs=1) as keep:
+    with tc.manual_schedule(), tc.tile_pool(name="keep", bufs=1) as keep:
         ident = keep.tile([P, P], F32)
         make_identity(nc, ident[:])
         emb_t = keep.tile([P, D_CHUNKS, B], F32)

@@ -93,10 +93,11 @@ def embed(tc, ident, emb_t, lab_t, sbj_vec, obj_vec, W1_words, W1_scales, b1, W2
             nc.sync.dma_start(out=x_rows[i][:, 0:DH], in_=sbj_vec[b_rows, :])
             nc.sync.dma_start(out=x_rows[i][:, DH:K1], in_=obj_vec[b_rows, :])
 
-        b1_all = fixed.tile([P, DO], BF16)
-        nc.scalar.dma_start(out=b1_all[:], in_=b1.partition_broadcast(P))
         for i in range(AHEAD):
             load_x(i)
+        b1_row = fixed.tile([P, DO], BF16)
+        nc.vector.memset(b1_row[:], 0.0)
+        nc.sync.dma_start(out=b1_row[0:1, :], in_=b1.rearrange("(o n) -> o n", o=1))
         lab_rows = fixed.tile([P, DO], BF16)
         nc.sync.dma_start(out=lab_rows[:], in_=label_vecs)
         b2_rows = fixed.tile([P, P], BF16)
@@ -124,6 +125,17 @@ def embed(tc, ident, emb_t, lab_t, sbj_vec, obj_vec, W1_words, W1_scales, b1, W2
                 scales=x_scales[i][:].rearrange("p g r -> p (g r)"),
                 in_=x_grouped[i][:].rearrange("p g r t -> p (g r t)"),
             )
+
+        b1_all = fixed.tile([P, DO], F32)
+
+        def spread_b1():
+            ones = fixed.tile([P, P], BF16)
+            nc.vector.memset(ones[:], 1.0)
+            for n in range(DO // N_MOVING):
+                n_cols = slice(n * N_MOVING, (n + 1) * N_MOVING)
+                bank = sums.tile([P, N_MOVING], F32, name="acc")
+                nc.tensor.matmul(out=bank[:], lhsT=ones[:], rhs=b1_row[:, n_cols], start=True, stop=True)
+                nc.vector.tensor_copy(out=b1_all[:, n_cols], in_=bank[:])
 
         b2_t = fixed.tile([P, D_CHUNKS], F32)
 
@@ -210,6 +222,7 @@ def embed(tc, ident, emb_t, lab_t, sbj_vec, obj_vec, W1_words, W1_scales, b1, W2
             turn_x(i)
         quantise_x(0)
         turn_labels_and_b2()
+        spread_b1()
         for i in range(1, AHEAD):
             quantise_x(i)
         for i in range(B_TILES):
@@ -235,6 +248,7 @@ HALVES = D_CHUNKS // HALF_CHUNKS
 QUARTET = 4
 QUARTETS = B_TILES // QUARTET
 STATS = 6
+LABEL_BLOCK = 32
 SQRT_FLOOR = 1e-30
 
 
@@ -242,12 +256,14 @@ def label_distances(tc, ident, emb_t, lab_t, out):
     nc = tc.nc
     with ExitStack() as ctx:
         fixed = ctx.enter_context(tc.tile_pool(name="results", bufs=1))
-        diffs = ctx.enter_context(tc.tile_pool(name="diffs", bufs=3))
+        diffs = ctx.enter_context(tc.tile_pool(name="diffs", bufs=3, reuse_waits="tile"))
         waste = ctx.enter_context(tc.tile_pool(name="waste", bufs=2))
-        banks = ctx.enter_context(tc.psum_pool(name="banks", bufs=8))
+        banks = ctx.enter_context(tc.psum_pool(name="banks", bufs=8, reuse_waits="tile"))
 
         by_scalar = fixed.tile([P, HALVES, QUARTETS, QUARTET - 1, L], F32)
         by_vector = fixed.tile([P, QUARTETS, L, HALVES, STATS], F32)
+        parts = fixed.tile([P, QUARTETS, L, 2 * HALVES], F32)
+        total = fixed.tile([P, QUARTETS, QUARTET, L], F32)
 
         def clip_differences(diff, step, chunks):
             label, half = step
@@ -261,6 +277,17 @@ def label_distances(tc, ident, emb_t, lab_t, out):
                     op0=ALU.subtract,
                     op1=ALU.min,
                 )
+
+        def totals_from_stats(labels):
+            triples = by_vector[:, :, labels, :, :].rearrange("p q l h (e s) -> p q l (h e) s", s=3)
+            mean, spread = triples[:, :, :, :, 1], triples[:, :, :, :, 2]
+            some = parts[:, :, labels, :]
+            nc.vector.tensor_tensor(out=some, in0=mean, in1=mean, op=ALU.mult)
+            nc.vector.tensor_scalar_mul(out=some, in0=some, scalar1=float(HALF_CHUNKS * P // 2))
+            nc.vector.tensor_tensor(out=some, in0=some, in1=spread, op=ALU.add)
+            nc.vector.tensor_reduce(
+                out=total[:, :, QUARTET - 1, labels], in_=some, axis=mybir.AxisListType.X, op=ALU.add
+            )
 
         steps = [(label, half) for label in range(L) for half in range(HALVES)]
         per_quartet = HALF_CHUNKS // QUARTETS
@@ -292,27 +319,17 @@ def label_distances(tc, ident, emb_t, lab_t, out):
                         nc.vector.bn_stats(out=by_vector[:, quartet, label, half, :], in_=bank[:])
             if following is not None:
                 diff = diff_next
+            if (s + 1) % (HALVES * LABEL_BLOCK) == 0:
+                totals_from_stats(slice(label + 1 - LABEL_BLOCK, label + 1))
 
-        total = fixed.tile([P, QUARTETS, QUARTET, L], F32)
         nc.vector.tensor_tensor(
-            out=total[:, :, 0 : QUARTET - 1, :], in0=by_scalar[:, 0, :, :, :], in1=by_scalar[:, 1, :, :, :], op=ALU.add
-        )
-        stats = by_vector[:].rearrange("p q l h (e s) -> p (q l) (h e) s", s=3)
-        parts = fixed.tile([P, QUARTETS * L, 2 * HALVES], F32)
-        count = float(HALF_CHUNKS * P // 2)
-        nc.vector.tensor_tensor(out=parts[:], in0=stats[:, :, :, 1], in1=stats[:, :, :, 1], op=ALU.mult)
-        nc.vector.tensor_scalar_mul(out=parts[:], in0=parts[:], scalar1=count)
-        nc.vector.tensor_tensor(out=parts[:], in0=parts[:], in1=stats[:, :, :, 2], op=ALU.add)
-        nc.vector.tensor_reduce(
-            out=total[:, :, QUARTET - 1, :],
-            in_=parts[:].rearrange("p (q l) s -> p q l s", q=QUARTETS),
-            axis=mybir.AxisListType.X,
+            out=total[:, :, 0 : QUARTET - 1, :],
+            in0=by_scalar[:, 0, :, :, :],
+            in1=by_scalar[:, 1, :, :, :],
             op=ALU.add,
         )
-
-        nc.vector.tensor_scalar_max(out=total[:], in0=total[:], scalar1=SQRT_FLOOR)
         scores = fixed.tile([P, QUARTETS, QUARTET, L], F32)
-        nc.scalar.activation(out=scores[:], in_=total[:], func=ACT.Sqrt)
+        nc.scalar.activation(out=scores[:], in_=total[:], func=ACT.Sqrt, bias=SQRT_FLOOR)
         nc.vector.tensor_scalar_mul(out=scores[:], in0=scores[:], scalar1=-1.0)
         nc.sync.dma_start(
             out=out.rearrange("(t p) l -> p t l", p=P), in_=scores[:].rearrange("p q i l -> p (q i) l")
@@ -326,6 +343,9 @@ def tile_relationembedding_kernel(
     with tc.manual_schedule(), tc.tile_pool(name="keep", bufs=1) as keep:
         ident = keep.tile([P, P], F32)
         make_identity(nc, ident[:])
+        one = keep.tile([P, 1], F32)
+        nc.vector.memset(one[:], 1.0)
+        nc.scalar.activation(out=one[:], in_=one[:], func=ACT.Sqrt)
         emb_t = keep.tile([P, D_CHUNKS, B], F32)
         lab_t = keep.tile([P, D_CHUNKS, L], F32)
         embed(

@@ -249,6 +249,7 @@ QUARTET = 4
 QUARTETS = B_TILES // QUARTET
 STATS = 6
 LABEL_BLOCK = 32
+STEPS_AHEAD = 2
 SQRT_FLOOR = 1e-30
 
 
@@ -256,7 +257,7 @@ def label_distances(tc, ident, emb_t, lab_t, out):
     nc = tc.nc
     with ExitStack() as ctx:
         fixed = ctx.enter_context(tc.tile_pool(name="results", bufs=1))
-        diffs = ctx.enter_context(tc.tile_pool(name="diffs", bufs=3, reuse_waits="tile"))
+        diffs = ctx.enter_context(tc.tile_pool(name="diffs", bufs=STEPS_AHEAD + 2, reuse_waits="tile"))
         waste = ctx.enter_context(tc.tile_pool(name="waste", bufs=2))
         banks = ctx.enter_context(tc.psum_pool(name="banks", bufs=8, reuse_waits="tile"))
 
@@ -291,12 +292,16 @@ def label_distances(tc, ident, emb_t, lab_t, out):
 
         steps = [(label, half) for label in range(L) for half in range(HALVES)]
         per_quartet = HALF_CHUNKS // QUARTETS
-        diff = diffs.tile([P, HALF_CHUNKS, B], F32, name="diff")
-        clip_differences(diff, steps[0], range(HALF_CHUNKS))
+        diff_of = {}
+        for s in range(STEPS_AHEAD):
+            diff_of[s] = diffs.tile([P, HALF_CHUNKS, B], F32, name="diff")
+            clip_differences(diff_of[s], steps[s], range(HALF_CHUNKS))
         for s, (label, half) in enumerate(steps):
-            following = steps[s + 1] if s + 1 < len(steps) else None
+            diff = diff_of[s]
+            following = steps[s + STEPS_AHEAD] if s + STEPS_AHEAD < len(steps) else None
             if following is not None:
                 diff_next = diffs.tile([P, HALF_CHUNKS, B], F32, name="diff")
+                diff_of[s + STEPS_AHEAD] = diff_next
             for quartet in range(QUARTETS):
                 if following is not None:
                     clip_differences(
@@ -317,8 +322,6 @@ def label_distances(tc, ident, emb_t, lab_t, out):
                         )
                     else:
                         nc.vector.bn_stats(out=by_vector[:, quartet, label, half, :], in_=bank[:])
-            if following is not None:
-                diff = diff_next
             if (s + 1) % (HALVES * LABEL_BLOCK) == 0:
                 totals_from_stats(slice(label + 1 - LABEL_BLOCK, label + 1))
 

@@ -230,16 +230,17 @@ def embed(tc, ident, emb_t, lab_t, sbj_vec, obj_vec, W1_words, W1_scales, b1, W2
             if later < B_TILES:
                 relu_x(later)
             first_layer(i)
+            if i > 0:
+                turn_hidden(i - 1)
+                if i * P % N_MOVING == 0:
+                    quantise_hidden(i * P // N_MOVING - 1)
             if later < B_TILES:
                 turn_x(later)
-            else:
-                share = D_CHUNKS // AHEAD
-                second_layer(0, range((later - B_TILES) * share, (later - B_TILES + 1) * share))
-            turn_hidden(i)
-            if later < B_TILES:
                 quantise_x(later)
-            if (i + 1) * P % N_MOVING == 0:
-                quantise_hidden(i * P // N_MOVING)
+        second_layer(0, range(0, D_CHUNKS // 2))
+        turn_hidden(B_TILES - 1)
+        second_layer(0, range(D_CHUNKS // 2, D_CHUNKS))
+        quantise_hidden(B // N_MOVING - 1)
         second_layer(1, range(D_CHUNKS))
 
 
@@ -248,7 +249,7 @@ HALVES = D_CHUNKS // HALF_CHUNKS
 QUARTET = 4
 QUARTETS = B_TILES // QUARTET
 STATS = 6
-LABEL_BLOCK = 32
+BLOCK_ENDS = (32, 64, 96, 120, 128)
 STEPS_AHEAD = 2
 SQRT_FLOOR = 1e-30
 
@@ -290,6 +291,36 @@ def label_distances(tc, ident, emb_t, lab_t, out):
                 out=total[:, :, QUARTET - 1, labels], in_=some, axis=mybir.AxisListType.X, op=ALU.add
             )
 
+        scores = fixed.tile([P, QUARTETS, QUARTET, L], F32)
+
+        def add_halves(labels):
+            nc.vector.tensor_tensor(
+                out=total[:, :, 0 : QUARTET - 1, labels],
+                in0=by_scalar[:, 0, :, :, labels],
+                in1=by_scalar[:, 1, :, :, labels],
+                op=ALU.add,
+            )
+
+        def take_root(labels):
+            nc.scalar.activation(
+                out=scores[:, :, :, labels], in_=total[:, :, :, labels], func=ACT.Sqrt, bias=SQRT_FLOOR
+            )
+
+        def negate_and_store(labels):
+            nc.vector.tensor_scalar_mul(out=scores[:, :, :, labels], in0=scores[:, :, :, labels], scalar1=-1.0)
+            nc.sync.dma_start(
+                out=out.rearrange("(t p) l -> p t l", p=P)[:, :, labels],
+                in_=scores[:].rearrange("p q i l -> p (q i) l")[:, :, labels],
+            )
+
+        finishing = (totals_from_stats, add_halves, take_root, negate_and_store)
+        due = {}
+        first = 0
+        for last in BLOCK_ENDS:
+            for stage, work in enumerate(finishing):
+                due.setdefault(last * HALVES - 1 + stage, []).append((work, slice(first, last)))
+            first = last
+
         steps = [(label, half) for label in range(L) for half in range(HALVES)]
         per_quartet = HALF_CHUNKS // QUARTETS
         diff_of = {}
@@ -322,21 +353,11 @@ def label_distances(tc, ident, emb_t, lab_t, out):
                         )
                     else:
                         nc.vector.bn_stats(out=by_vector[:, quartet, label, half, :], in_=bank[:])
-            if (s + 1) % (HALVES * LABEL_BLOCK) == 0:
-                totals_from_stats(slice(label + 1 - LABEL_BLOCK, label + 1))
-
-        nc.vector.tensor_tensor(
-            out=total[:, :, 0 : QUARTET - 1, :],
-            in0=by_scalar[:, 0, :, :, :],
-            in1=by_scalar[:, 1, :, :, :],
-            op=ALU.add,
-        )
-        scores = fixed.tile([P, QUARTETS, QUARTET, L], F32)
-        nc.scalar.activation(out=scores[:], in_=total[:], func=ACT.Sqrt, bias=SQRT_FLOOR)
-        nc.vector.tensor_scalar_mul(out=scores[:], in0=scores[:], scalar1=-1.0)
-        nc.sync.dma_start(
-            out=out.rearrange("(t p) l -> p t l", p=P), in_=scores[:].rearrange("p q i l -> p (q i) l")
-        )
+            for work, labels in due.get(s, []):
+                work(labels)
+        for s in range(len(steps), len(steps) + len(finishing)):
+            for work, labels in due.get(s, []):
+                work(labels)
 
 
 def tile_relationembedding_kernel(

@@ -111,7 +111,8 @@ def embed(tc, ident, emb_t, lab_t, sbj_vec, obj_vec, W1_words, W1_scales, b1, W2
         x_codes, x_scales, x_grouped = {}, {}, {}
 
         def relu_x(i):
-            nc.vector.tensor_scalar_max(out=x_rows[i][:], in0=x_rows[i][:], scalar1=0.0)
+            for part in (slice(0, DH), slice(DH, K1)):
+                nc.vector.tensor_scalar_max(out=x_rows[i][:, part], in0=x_rows[i][:, part], scalar1=0.0)
 
         def turn_x(i):
             x_grouped[i] = double.tile([P, passes_1, P, PACK], BF16, name="x_grouped", align_bytes=64)

@@ -345,7 +345,7 @@ def label_distances(tc, ident, emb_t, lab_t, out):
                     for j in range(HALF_CHUNKS):
                         nc.tensor.transpose(bank[:, j, :], diff[:, j, b_cols], ident)
                     if place < QUARTET - 1:
-                        squares = waste.tile([P, HALF_CHUNKS, P], F32, name="squares")
+                        squares = waste.tile([P, HALF_CHUNKS, P], BF16, name="squares")
                         nc.scalar.activation(
                             out=squares[:],
                             in_=bank[:],

@@ -245,13 +245,14 @@ def embed(tc, ident, emb_t, lab_t, sbj_vec, obj_vec, W1_words, W1_scales, b1, W2
         second_layer(1, range(D_CHUNKS))
 
 
-HALF_CHUNKS = TURNS_PER_BANK
-HALVES = D_CHUNKS // HALF_CHUNKS
-QUARTET = 4
-QUARTETS = B_TILES // QUARTET
+SETS = 3
+SET_CHUNKS = TURNS_PER_BANK
+PAIRS = L // 2
+S_TILES = 5
+V_TILES = B_TILES - S_TILES
 STATS = 6
-BLOCK_ENDS = (32, 64, 96, 120, 128)
-STEPS_AHEAD = 2
+PAIR_ENDS = (16, 32, 48, 60, 64)
+LOWEST = -3.4028234663852886e38
 SQRT_FLOOR = 1e-30
 
 
@@ -259,106 +260,182 @@ def label_distances(tc, ident, emb_t, lab_t, out):
     nc = tc.nc
     with ExitStack() as ctx:
         fixed = ctx.enter_context(tc.tile_pool(name="results", bufs=1))
-        diffs = ctx.enter_context(tc.tile_pool(name="diffs", bufs=STEPS_AHEAD + 2, reuse_waits="tile"))
+        diffs = ctx.enter_context(tc.tile_pool(name="diffs", bufs=4, reuse_waits="tile"))
+        mins = ctx.enter_context(tc.tile_pool(name="mins", bufs=4, reuse_waits="tile"))
+        squares = ctx.enter_context(tc.tile_pool(name="squares", bufs=8, reuse_waits="tile"))
         waste = ctx.enter_context(tc.tile_pool(name="waste", bufs=2))
-        banks = ctx.enter_context(tc.psum_pool(name="banks", bufs=8, reuse_waits="tile"))
+        floors = ctx.enter_context(tc.tile_pool(name="floors", bufs=2))
+        banks_s = ctx.enter_context(tc.psum_pool(name="banks_s", bufs=4, reuse_waits="tile"))
+        banks_v = ctx.enter_context(tc.psum_pool(name="banks_v", bufs=3, reuse_waits="tile"))
+        banks_q = ctx.enter_context(tc.psum_pool(name="banks_q", bufs=1, reuse_waits="tile"))
 
-        by_scalar = fixed.tile([P, HALVES, QUARTETS, QUARTET - 1, L], F32)
-        by_vector = fixed.tile([P, QUARTETS, L, HALVES, STATS], F32)
-        parts = fixed.tile([P, QUARTETS, L, 2 * HALVES], F32)
-        total = fixed.tile([P, QUARTETS, QUARTET, L], F32)
+        usum = fixed.tile([P, SETS, B_TILES, PAIRS], F32)
+        stats = fixed.tile([P, SETS * V_TILES, PAIRS, STATS], F32)
+        parts = fixed.tile([P, SETS * V_TILES, PAIRS, 2], F32)
+        total = fixed.tile([P, B_TILES, L], F32)
+        scores = fixed.tile([P, B_TILES, L], F32)
+        neg_lab = fixed.tile([P, D_CHUNKS, L], F32)
+        nc.vector.tensor_scalar_mul(out=neg_lab[:], in0=lab_t[:], scalar1=-1.0)
+        ones = fixed.tile([P, 1], F32)
+        nc.vector.memset(ones[:], 1.0)
 
-        def clip_differences(diff, step, chunks):
-            label, half = step
-            for j in chunks:
-                c = half * HALF_CHUNKS + j
-                nc.vector.tensor_scalar(
-                    out=diff[:, j, :],
+        diff_of, min_of, square_of, res_of = {}, {}, {}, {}
+
+        def clip(pair, which, j):
+            if (pair, which) not in diff_of:
+                diff_of[pair, which] = diffs.tile([P, SET_CHUNKS, B], F32, name="diff")
+            label = 2 * pair + min(which, 1)
+            c = j + SET_CHUNKS * max(which - 1, 0)
+            nc.vector.tensor_scalar(
+                out=diff_of[pair, which][:, j, :],
+                in0=emb_t[:, c, :],
+                scalar1=lab_t[:, c, label : label + 1],
+                scalar2=0.0,
+                op0=ALU.subtract,
+                op1=ALU.min,
+            )
+
+        def gpsimd_minima(pair, js):
+            lowest = floors.tile([P, 1], F32, name="lowest")
+            nc.vector.memset(lowest[:], LOWEST)
+            for j in js:
+                c = SET_CHUNKS + j
+                min_of[pair, j] = mins.tile([P, B], F32, name="minimum")
+                nc.gpsimd.tensor_scalar(
+                    out=min_of[pair, j][:],
                     in0=emb_t[:, c, :],
-                    scalar1=lab_t[:, c, label : label + 1],
-                    scalar2=0.0,
-                    op0=ALU.subtract,
-                    op1=ALU.min,
+                    scalar1=lab_t[:, c, 2 * pair : 2 * pair + 1],
+                    scalar2=lowest[:],
+                    op0=ALU.min,
+                    op1=ALU.max,
                 )
 
-        def totals_from_stats(labels):
-            triples = by_vector[:, :, labels, :, :].rearrange("p q l h (e s) -> p q l (h e) s", s=3)
-            mean, spread = triples[:, :, :, :, 1], triples[:, :, :, :, 2]
-            some = parts[:, :, labels, :]
-            nc.vector.tensor_tensor(out=some, in0=mean, in1=mean, op=ALU.mult)
-            nc.vector.tensor_scalar_mul(out=some, in0=some, scalar1=float(HALF_CHUNKS * P // 2))
-            nc.vector.tensor_tensor(out=some, in0=some, in1=spread, op=ALU.add)
-            nc.vector.tensor_reduce(
-                out=total[:, :, QUARTET - 1, labels], in_=some, axis=mybir.AxisListType.X, op=ALU.add
+        def square(pair, j):
+            c = SET_CHUNKS + j
+            square_of[pair, j] = squares.tile([P, B], F32, name="square")
+            nc.scalar.activation(
+                out=square_of[pair, j][:],
+                in_=min_of[pair, j][:],
+                func=ACT.Square,
+                bias=neg_lab[:, c, 2 * pair : 2 * pair + 1],
             )
 
-        scores = fixed.tile([P, QUARTETS, QUARTET, L], F32)
+        def sum_squares(pair, tile):
+            first = max(e for e in (0,) + PAIR_ENDS if e <= pair)
+            if first not in res_of:
+                res_of[first] = banks_q.tile([P, PAIR_ENDS[0], B_TILES], F32, name="res")
+            for j in range(SET_CHUNKS):
+                nc.tensor.matmul(
+                    out=res_of[first][:, pair - first, tile : tile + 1],
+                    lhsT=square_of[pair, j][:, tile * P : (tile + 1) * P],
+                    rhs=ones[:],
+                    start=(j == 0),
+                    stop=(j == SET_CHUNKS - 1),
+                )
 
-        def add_halves(labels):
+        def turn(pool, pair, which, tile):
+            bank = pool.tile([P, SET_CHUNKS, P], F32, name="bank")
+            for j in range(SET_CHUNKS):
+                nc.tensor.transpose(bank[:, j, :], diff_of[pair, which][:, j, tile * P : (tile + 1) * P], ident)
+            return bank
+
+        def bank_work(pair, which, tile):
+            if tile < S_TILES:
+                bank = turn(banks_s, pair, which, tile)
+                unread = waste.tile([P, SET_CHUNKS, P], BF16, name="unread")
+                nc.scalar.activation(
+                    out=unread[:], in_=bank[:], func=ACT.Square, accum_out=usum[:, which, tile, pair : pair + 1]
+                )
+            else:
+                bank = turn(banks_v, pair, which, tile)
+                nc.vector.bn_stats(out=stats[:, which * V_TILES + tile - S_TILES, pair, :], in_=bank[:])
+
+        def totals(pairs):
+            res = res_of[pairs.start]
+            width = pairs.stop - pairs.start
+            labels_a = slice(2 * pairs.start, 2 * pairs.stop, 2)
+            labels_b = slice(2 * pairs.start + 1, 2 * pairs.stop, 2)
+            triples = stats[:, :, pairs, :].rearrange("p q n (e s) -> p q n e s", s=3)
+            mean, spread = triples[:, :, :, :, 1], triples[:, :, :, :, 2]
+            some = parts[:, :, pairs, :]
+            nc.vector.tensor_tensor(out=some, in0=mean, in1=mean, op=ALU.mult)
+            nc.vector.tensor_scalar_mul(out=some, in0=some, scalar1=float(SET_CHUNKS * P // 2))
+            nc.vector.tensor_tensor(out=some, in0=some, in1=spread, op=ALU.add)
+            halves = some.rearrange("p (w t) n e -> p w t n e", t=V_TILES)
             nc.vector.tensor_tensor(
-                out=total[:, :, 0 : QUARTET - 1, labels],
-                in0=by_scalar[:, 0, :, :, labels],
-                in1=by_scalar[:, 1, :, :, labels],
+                out=usum[:, :, S_TILES:, pairs], in0=halves[:, :, :, :, 0], in1=halves[:, :, :, :, 1], op=ALU.add
+            )
+            nc.vector.tensor_tensor(
+                out=total[:, :, labels_a],
+                in0=usum[:, 0, :, pairs],
+                in1=res[:, 0:width, :].rearrange("p n t -> p t n"),
                 op=ALU.add,
             )
+            nc.vector.tensor_tensor(
+                out=total[:, :, labels_b], in0=usum[:, 1, :, pairs], in1=usum[:, 2, :, pairs], op=ALU.add
+            )
 
-        def take_root(labels):
+        def take_root(pairs):
+            labels = slice(2 * pairs.start, 2 * pairs.stop)
             nc.scalar.activation(
-                out=scores[:, :, :, labels], in_=total[:, :, :, labels], func=ACT.Sqrt, bias=SQRT_FLOOR
+                out=scores[:, :, labels], in_=total[:, :, labels], func=ACT.Sqrt, bias=SQRT_FLOOR
             )
 
-        def negate_and_store(labels):
-            nc.vector.tensor_scalar_mul(out=scores[:, :, :, labels], in0=scores[:, :, :, labels], scalar1=-1.0)
+        def negate_and_store(pairs):
+            labels = slice(2 * pairs.start, 2 * pairs.stop)
+            nc.vector.tensor_scalar_mul(out=scores[:, :, labels], in0=scores[:, :, labels], scalar1=-1.0)
             nc.sync.dma_start(
-                out=out.rearrange("(t p) l -> p t l", p=P)[:, :, labels],
-                in_=scores[:].rearrange("p q i l -> p (q i) l")[:, :, labels],
+                out=out.rearrange("(t p) l -> p t l", p=P)[:, :, labels], in_=scores[:, :, labels]
             )
 
-        finishing = (totals_from_stats, add_halves, take_root, negate_and_store)
         due = {}
         first = 0
-        for last in BLOCK_ENDS:
-            for stage, work in enumerate(finishing):
-                due.setdefault(last * HALVES - 1 + stage, []).append((work, slice(first, last)))
+        for last in PAIR_ENDS:
+            for stage, work in enumerate((totals, take_root, negate_and_store)):
+                due.setdefault(2 * last + min(1, PAIRS - last) + stage, []).append((work, slice(first, last)))
             first = last
 
-        steps = [(label, half) for label in range(L) for half in range(HALVES)]
-        per_quartet = HALF_CHUNKS // QUARTETS
-        diff_of = {}
-        for s in range(STEPS_AHEAD):
-            diff_of[s] = diffs.tile([P, HALF_CHUNKS, B], F32, name="diff")
-            clip_differences(diff_of[s], steps[s], range(HALF_CHUNKS))
-        for s, (label, half) in enumerate(steps):
-            diff = diff_of[s]
-            following = steps[s + STEPS_AHEAD] if s + STEPS_AHEAD < len(steps) else None
-            if following is not None:
-                diff_next = diffs.tile([P, HALF_CHUNKS, B], F32, name="diff")
-                diff_of[s + STEPS_AHEAD] = diff_next
-            for quartet in range(QUARTETS):
-                if following is not None:
-                    clip_differences(
-                        diff_next, following, range(quartet * per_quartet, (quartet + 1) * per_quartet)
-                    )
-                for place in range(QUARTET):
-                    b_cols = slice((quartet * QUARTET + place) * P, (quartet * QUARTET + place + 1) * P)
-                    bank = banks.tile([P, HALF_CHUNKS, P], F32, name="bank")
-                    for j in range(HALF_CHUNKS):
-                        nc.tensor.transpose(bank[:, j, :], diff[:, j, b_cols], ident)
-                    if place < QUARTET - 1:
-                        squares = waste.tile([P, HALF_CHUNKS, P], BF16, name="squares")
-                        nc.scalar.activation(
-                            out=squares[:],
-                            in_=bank[:],
-                            func=ACT.Square,
-                            accum_out=by_scalar[:, half, quartet, place, label : label + 1],
-                        )
-                    else:
-                        nc.vector.bn_stats(out=by_vector[:, quartet, label, half, :], in_=bank[:])
-            for work, labels in due.get(s, []):
-                work(labels)
-        for s in range(len(steps), len(steps) + len(finishing)):
-            for work, labels in due.get(s, []):
-                work(labels)
+        order = (
+            [(0, t) for t in (0, 1, 5, 2, 3, 6, 4, 7)] + [(1, t) for t in (0, 5, 1, 6)],
+            [(1, t) for t in (2, 3, 7, 4)] + [(2, t) for t in (0, 5, 1, 6, 2, 7, 3, 4)],
+        )
+        for which in (0, 1):
+            for j in range(SET_CHUNKS):
+                clip(0, which, j)
+        gpsimd_minima(0, range(SET_CHUNKS))
+        to_square = [(0, 0), (0, 1), (0, 2), (0, 3)]
+        to_sum = []
+        for s in range(2 * PAIRS):
+            pair, half = s // 2, s % 2
+            clips = (
+                [(pair, 2, j) for j in range(SET_CHUNKS)] + [(pair + 1, 0, j) for j in (0, 1)]
+                if half == 0
+                else [(pair + 1, 0, j) for j in (2, 3)] + [(pair + 1, 1, j) for j in range(SET_CHUNKS)]
+            )
+            for i, (p, which, j) in enumerate(clips):
+                if p < PAIRS:
+                    clip(p, which, j)
+                if i == 1:
+                    for work, pairs in due.get(s, []):
+                        work(pairs)
+            if pair + 1 < PAIRS:
+                gpsimd_minima(pair + 1, (2 * half, 2 * half + 1))
+            if half == 1:
+                to_sum.extend((pair, t) for t in range(B_TILES))
+            sums_now = len(to_sum) if s == 2 * PAIRS - 1 else min(4, len(to_sum))
+            for i, (which, tile) in enumerate(order[half]):
+                if i in (2, 6) or (i in (4, 8) and s == 0):
+                    if to_square:
+                        square(*to_square.pop(0))
+                bank_work(pair, which, tile)
+                if i % 3 == 2:
+                    for k in range(sums_now // 4):
+                        sum_squares(*to_sum.pop(0))
+            if pair + 1 < PAIRS:
+                to_square.extend((pair + 1, j) for j in (2 * half, 2 * half + 1))
+        for s in range(2 * PAIRS, 2 * PAIRS + 4):
+            for work, pairs in due.get(s, []):
+                work(pairs)
 
 
 def tile_relationembedding_kernel(

@@ -245,15 +245,18 @@ def embed(tc, ident, emb_t, lab_t, sbj_vec, obj_vec, W1_words, W1_scales, b1, W2
         second_layer(1, range(D_CHUNKS))
 
 
-SETS = 3
 SET_CHUNKS = TURNS_PER_BANK
-PAIRS = L // 2
+HALVES = D_CHUNKS // SET_CHUNKS
+GROUP = 4
+OTHERS = GROUP - 1
+GROUPS = L // GROUP
 S_TILES = 5
 V_TILES = B_TILES - S_TILES
 STATS = 6
-PAIR_ENDS = (16, 32, 48, 60, 64)
+GROUP_ENDS = (8, 16, 24, 30, 32)
 LOWEST = -3.4028234663852886e38
 SQRT_FLOOR = 1e-30
+QUARTERS = 4
 
 
 def label_distances(tc, ident, emb_t, lab_t, out):
@@ -262,32 +265,35 @@ def label_distances(tc, ident, emb_t, lab_t, out):
         fixed = ctx.enter_context(tc.tile_pool(name="results", bufs=1))
         diffs = ctx.enter_context(tc.tile_pool(name="diffs", bufs=4, reuse_waits="tile"))
         mins = ctx.enter_context(tc.tile_pool(name="mins", bufs=4, reuse_waits="tile"))
-        squares = ctx.enter_context(tc.tile_pool(name="squares", bufs=8, reuse_waits="tile"))
+        squares = ctx.enter_context(tc.tile_pool(name="squares", bufs=16, reuse_waits="tile"))
         waste = ctx.enter_context(tc.tile_pool(name="waste", bufs=2))
         floors = ctx.enter_context(tc.tile_pool(name="floors", bufs=2))
         banks_s = ctx.enter_context(tc.psum_pool(name="banks_s", bufs=4, reuse_waits="tile"))
         banks_v = ctx.enter_context(tc.psum_pool(name="banks_v", bufs=3, reuse_waits="tile"))
         banks_q = ctx.enter_context(tc.psum_pool(name="banks_q", bufs=1, reuse_waits="tile"))
 
-        usum = fixed.tile([P, SETS, B_TILES, PAIRS], F32)
-        stats = fixed.tile([P, SETS * V_TILES, PAIRS, STATS], F32)
-        parts = fixed.tile([P, SETS * V_TILES, PAIRS, 2], F32)
+        usum = fixed.tile([P, HALVES, B_TILES, OTHERS * GROUPS], F32)
+        stats = fixed.tile([P, HALVES * V_TILES, OTHERS * GROUPS, STATS], F32)
+        parts = fixed.tile([P, HALVES * V_TILES, OTHERS * GROUPS, 2], F32)
         total = fixed.tile([P, B_TILES, L], F32)
         scores = fixed.tile([P, B_TILES, L], F32)
-        neg_lab = fixed.tile([P, D_CHUNKS, L], F32)
-        nc.vector.tensor_scalar_mul(out=neg_lab[:], in0=lab_t[:], scalar1=-1.0)
-        ones = fixed.tile([P, 1], F32)
-        nc.vector.memset(ones[:], 1.0)
+        neg_lab = fixed.tile([P, D_CHUNKS, GROUPS], F32)
+        nc.vector.tensor_scalar_mul(
+            out=neg_lab[:], in0=lab_t[:].rearrange("p c (n u) -> p c n u", u=GROUP)[:, :, :, 0], scalar1=-1.0
+        )
 
-        diff_of, min_of, square_of, res_of = {}, {}, {}, {}
+        sets = [(GROUP * n + u, half) for n in range(GROUPS) for u in range(1, GROUP) for half in range(HALVES)]
+        clip_list = [(q, j) for q in range(len(sets)) for j in range(SET_CHUNKS)]
+        minima_list = [(n, c) for n in range(GROUPS) for c in range(D_CHUNKS)]
+        diff_of, min_of, square_of, acc_of = {}, {}, {}, {}
 
-        def clip(pair, which, j):
-            if (pair, which) not in diff_of:
-                diff_of[pair, which] = diffs.tile([P, SET_CHUNKS, B], F32, name="diff")
-            label = 2 * pair + min(which, 1)
-            c = j + SET_CHUNKS * max(which - 1, 0)
+        def clip(q, j):
+            label, half = sets[q]
+            if q not in diff_of:
+                diff_of[q] = diffs.tile([P, SET_CHUNKS, B], F32, name="diff")
+            c = half * SET_CHUNKS + j
             nc.vector.tensor_scalar(
-                out=diff_of[pair, which][:, j, :],
+                out=diff_of[q][:, j, :],
                 in0=emb_t[:, c, :],
                 scalar1=lab_t[:, c, label : label + 1],
                 scalar2=0.0,
@@ -295,94 +301,95 @@ def label_distances(tc, ident, emb_t, lab_t, out):
                 op1=ALU.min,
             )
 
-        def gpsimd_minima(pair, js):
+        def minima(items):
             lowest = floors.tile([P, 1], F32, name="lowest")
             nc.vector.memset(lowest[:], LOWEST)
-            for j in js:
-                c = SET_CHUNKS + j
-                min_of[pair, j] = mins.tile([P, B], F32, name="minimum")
+            for n, c in items:
+                min_of[n, c] = mins.tile([P, B], F32, name="minimum")
                 nc.gpsimd.tensor_scalar(
-                    out=min_of[pair, j][:],
+                    out=min_of[n, c][:],
                     in0=emb_t[:, c, :],
-                    scalar1=lab_t[:, c, 2 * pair : 2 * pair + 1],
+                    scalar1=lab_t[:, c, GROUP * n : GROUP * n + 1],
                     scalar2=lowest[:],
                     op0=ALU.min,
                     op1=ALU.max,
                 )
 
-        def square(pair, j):
-            c = SET_CHUNKS + j
-            square_of[pair, j] = squares.tile([P, B], F32, name="square")
+        def square(n, c):
+            square_of[n, c] = squares.tile([P, B], F32, name="square")
             nc.scalar.activation(
-                out=square_of[pair, j][:],
-                in_=min_of[pair, j][:],
-                func=ACT.Square,
-                bias=neg_lab[:, c, 2 * pair : 2 * pair + 1],
+                out=square_of[n, c][:], in_=min_of[n, c][:], func=ACT.Square, bias=neg_lab[:, c, n : n + 1]
             )
 
-        def sum_squares(pair, tile):
-            first = max(e for e in (0,) + PAIR_ENDS if e <= pair)
-            if first not in res_of:
-                res_of[first] = banks_q.tile([P, PAIR_ENDS[0], B_TILES], F32, name="res")
-            for j in range(SET_CHUNKS):
+        def sum_over_chunks(n, tile):
+            bank = tile // SET_CHUNKS
+            if (n, bank) not in acc_of:
+                acc_of[n, bank] = banks_q.tile([P, SET_CHUNKS, P], F32, name="acc_q")
+            for c in range(D_CHUNKS):
                 nc.tensor.matmul(
-                    out=res_of[first][:, pair - first, tile : tile + 1],
-                    lhsT=square_of[pair, j][:, tile * P : (tile + 1) * P],
-                    rhs=ones[:],
-                    start=(j == 0),
-                    stop=(j == SET_CHUNKS - 1),
+                    out=acc_of[n, bank][:, tile % SET_CHUNKS, :],
+                    lhsT=square_of[n, c][:, tile * P : (tile + 1) * P],
+                    rhs=ident,
+                    is_transpose=True,
+                    start=(c == 0),
+                    stop=(c == D_CHUNKS - 1),
                 )
 
-        def turn(pool, pair, which, tile):
+        def sum_bank(n, bank):
+            nc.vector.tensor_reduce(
+                out=total[:, bank * SET_CHUNKS : (bank + 1) * SET_CHUNKS, GROUP * n : GROUP * n + 1],
+                in_=acc_of[n, bank][:],
+                axis=mybir.AxisListType.X,
+                op=ALU.add,
+            )
+
+        def turn(pool, q, tile):
             bank = pool.tile([P, SET_CHUNKS, P], F32, name="bank")
             for j in range(SET_CHUNKS):
-                nc.tensor.transpose(bank[:, j, :], diff_of[pair, which][:, j, tile * P : (tile + 1) * P], ident)
+                nc.tensor.transpose(bank[:, j, :], diff_of[q][:, j, tile * P : (tile + 1) * P], ident)
             return bank
 
-        def bank_work(pair, which, tile):
+        def bank_work(q, tile):
+            label, half = sets[q]
+            place = OTHERS * (label // GROUP) + label % GROUP - 1
             if tile < S_TILES:
-                bank = turn(banks_s, pair, which, tile)
+                bank = turn(banks_s, q, tile)
                 unread = waste.tile([P, SET_CHUNKS, P], BF16, name="unread")
                 nc.scalar.activation(
-                    out=unread[:], in_=bank[:], func=ACT.Square, accum_out=usum[:, which, tile, pair : pair + 1]
+                    out=unread[:], in_=bank[:], func=ACT.Square, accum_out=usum[:, half, tile, place : place + 1]
                 )
             else:
-                bank = turn(banks_v, pair, which, tile)
-                nc.vector.bn_stats(out=stats[:, which * V_TILES + tile - S_TILES, pair, :], in_=bank[:])
+                bank = turn(banks_v, q, tile)
+                nc.vector.bn_stats(out=stats[:, half * V_TILES + tile - S_TILES, place, :], in_=bank[:])
 
-        def totals(pairs):
-            res = res_of[pairs.start]
-            width = pairs.stop - pairs.start
-            labels_a = slice(2 * pairs.start, 2 * pairs.stop, 2)
-            labels_b = slice(2 * pairs.start + 1, 2 * pairs.stop, 2)
-            triples = stats[:, :, pairs, :].rearrange("p q n (e s) -> p q n e s", s=3)
+        def totals(groups):
+            places = slice(OTHERS * groups.start, OTHERS * groups.stop)
+            labels = slice(GROUP * groups.start, GROUP * groups.stop)
+            triples = stats[:, :, places, :].rearrange("p q n (e s) -> p q n e s", s=3)
             mean, spread = triples[:, :, :, :, 1], triples[:, :, :, :, 2]
-            some = parts[:, :, pairs, :]
+            some = parts[:, :, places, :]
             nc.vector.tensor_tensor(out=some, in0=mean, in1=mean, op=ALU.mult)
             nc.vector.tensor_scalar_mul(out=some, in0=some, scalar1=float(SET_CHUNKS * P // 2))
             nc.vector.tensor_tensor(out=some, in0=some, in1=spread, op=ALU.add)
             halves = some.rearrange("p (w t) n e -> p w t n e", t=V_TILES)
             nc.vector.tensor_tensor(
-                out=usum[:, :, S_TILES:, pairs], in0=halves[:, :, :, :, 0], in1=halves[:, :, :, :, 1], op=ALU.add
+                out=usum[:, :, S_TILES:, places], in0=halves[:, :, :, :, 0], in1=halves[:, :, :, :, 1], op=ALU.add
             )
             nc.vector.tensor_tensor(
-                out=total[:, :, labels_a],
-                in0=usum[:, 0, :, pairs],
-                in1=res[:, 0:width, :].rearrange("p n t -> p t n"),
+                out=total[:, :, labels].rearrange("p t (n u) -> p t n u", u=GROUP)[:, :, :, 1:],
+                in0=usum[:, 0, :, places].rearrange("p t (n u) -> p t n u", u=OTHERS),
+                in1=usum[:, 1, :, places].rearrange("p t (n u) -> p t n u", u=OTHERS),
                 op=ALU.add,
             )
-            nc.vector.tensor_tensor(
-                out=total[:, :, labels_b], in0=usum[:, 1, :, pairs], in1=usum[:, 2, :, pairs], op=ALU.add
-            )
 
-        def take_root(pairs):
-            labels = slice(2 * pairs.start, 2 * pairs.stop)
+        def take_root(groups):
+            labels = slice(GROUP * groups.start, GROUP * groups.stop)
             nc.scalar.activation(
                 out=scores[:, :, labels], in_=total[:, :, labels], func=ACT.Sqrt, bias=SQRT_FLOOR
             )
 
-        def negate_and_store(pairs):
-            labels = slice(2 * pairs.start, 2 * pairs.stop)
+        def negate_and_store(groups):
+            labels = slice(GROUP * groups.start, GROUP * groups.stop)
             nc.vector.tensor_scalar_mul(out=scores[:, :, labels], in0=scores[:, :, labels], scalar1=-1.0)
             nc.sync.dma_start(
                 out=out.rearrange("(t p) l -> p t l", p=P)[:, :, labels], in_=scores[:, :, labels]
@@ -390,52 +397,50 @@ def label_distances(tc, ident, emb_t, lab_t, out):
 
         due = {}
         first = 0
-        for last in PAIR_ENDS:
+        for last in GROUP_ENDS:
             for stage, work in enumerate((totals, take_root, negate_and_store)):
-                due.setdefault(2 * last + min(1, PAIRS - last) + stage, []).append((work, slice(first, last)))
+                due.setdefault(QUARTERS * last + (4 if last < GROUPS else 0) + stage, []).append((work, slice(first, last)))
             first = last
 
         order = (
             [(0, t) for t in (0, 1, 5, 2, 3, 6, 4, 7)] + [(1, t) for t in (0, 5, 1, 6)],
             [(1, t) for t in (2, 3, 7, 4)] + [(2, t) for t in (0, 5, 1, 6, 2, 7, 3, 4)],
         )
-        for which in (0, 1):
-            for j in range(SET_CHUNKS):
-                clip(0, which, j)
-        gpsimd_minima(0, range(SET_CHUNKS))
-        to_square = [(0, 0), (0, 1), (0, 2), (0, 3)]
-        to_sum = []
-        for s in range(2 * PAIRS):
-            pair, half = s // 2, s % 2
-            clips = (
-                [(pair, 2, j) for j in range(SET_CHUNKS)] + [(pair + 1, 0, j) for j in (0, 1)]
-                if half == 0
-                else [(pair + 1, 0, j) for j in (2, 3)] + [(pair + 1, 1, j) for j in range(SET_CHUNKS)]
-            )
-            for i, (p, which, j) in enumerate(clips):
-                if p < PAIRS:
-                    clip(p, which, j)
-                if i == 1:
-                    for work, pairs in due.get(s, []):
-                        work(pairs)
-            if pair + 1 < PAIRS:
-                gpsimd_minima(pair + 1, (2 * half, 2 * half + 1))
-            if half == 1:
-                to_sum.extend((pair, t) for t in range(B_TILES))
-            sums_now = len(to_sum) if s == 2 * PAIRS - 1 else min(4, len(to_sum))
-            for i, (which, tile) in enumerate(order[half]):
-                if i in (2, 6) or (i in (4, 8) and s == 0):
-                    if to_square:
-                        square(*to_square.pop(0))
-                bank_work(pair, which, tile)
-                if i % 3 == 2:
-                    for k in range(sums_now // 4):
-                        sum_squares(*to_sum.pop(0))
-            if pair + 1 < PAIRS:
-                to_square.extend((pair + 1, j) for j in (2 * half, 2 * half + 1))
-        for s in range(2 * PAIRS, 2 * PAIRS + 4):
-            for work, pairs in due.get(s, []):
-                work(pairs)
+        for item in clip_list[0:8]:
+            clip(*item)
+        minima(minima_list[0:4])
+        for s in range(QUARTERS * GROUPS):
+            clips = clip_list[8 + 6 * s : 14 + 6 * s]
+            for item in clips[0:2]:
+                clip(*item)
+            if s % 2 == 1 and s >= QUARTERS:
+                sum_bank(s // QUARTERS - 1, s % QUARTERS // 2)
+            for work, groups in due.get(s, []):
+                work(groups)
+            for item in clips[2:]:
+                clip(*item)
+            now = minima_list[4 + 2 * s : 6 + 2 * s]
+            if now:
+                minima(now)
+            pairs = minima_list[0:4] if s == 0 else minima_list[2 + 2 * s : 4 + 2 * s]
+            pairs = list(pairs)
+            n, k = (s - 3) // 4, (s - 3) % 4
+            tiles = [(n, 2 * k), (n, 2 * k + 1)] if n >= 0 else []
+            if s == QUARTERS * GROUPS - 1:
+                tiles = [(n, t) for t in range(B_TILES)]
+            for i, (which, tile) in enumerate(order[s % 2]):
+                if i in (2, 6) or (s == 0 and i in (4, 8)):
+                    if pairs:
+                        square(*pairs.pop(0))
+                bank_work(3 * (s // 2) + which, tile)
+                if i in (6, 10):
+                    for t in tiles[len(tiles) // 2 * (i == 10) : len(tiles) // 2 * (1 + (i == 10))]:
+                        sum_over_chunks(*t)
+                        if len(tiles) > 2 and t[1] % SET_CHUNKS == SET_CHUNKS - 1:
+                            sum_bank(n, t[1] // SET_CHUNKS)
+        for s in range(QUARTERS * GROUPS, QUARTERS * GROUPS + 4):
+            for work, groups in due.get(s, []):
+                work(groups)
 
 
 def tile_relationembedding_kernel(

@@ -301,14 +301,28 @@ def label_distances(tc, ident, emb_t, lab_t, out):
                 op1=ALU.min,
             )
 
-        def minima(items):
+        def share(item):
+            return B if item[1] % 2 == 0 else B // 2
+
+        def minima_by_vector(items):
+            for n, c in items:
+                min_of[n, c] = mins.tile([P, B], F32, name="minimum")
+                cols = slice(share((n, c)), B)
+                if cols.start < B:
+                    nc.vector.tensor_scalar_min(
+                        out=min_of[n, c][:, cols],
+                        in0=emb_t[:, c, cols],
+                        scalar1=lab_t[:, c, GROUP * n : GROUP * n + 1],
+                    )
+
+        def minima_by_gpsimd(items):
             lowest = floors.tile([P, 1], F32, name="lowest")
             nc.vector.memset(lowest[:], LOWEST)
             for n, c in items:
-                min_of[n, c] = mins.tile([P, B], F32, name="minimum")
+                cols = slice(0, share((n, c)))
                 nc.gpsimd.tensor_scalar(
-                    out=min_of[n, c][:],
-                    in0=emb_t[:, c, :],
+                    out=min_of[n, c][:, cols],
+                    in0=emb_t[:, c, cols],
                     scalar1=lab_t[:, c, GROUP * n : GROUP * n + 1],
                     scalar2=lowest[:],
                     op0=ALU.min,
@@ -399,7 +413,7 @@ def label_distances(tc, ident, emb_t, lab_t, out):
         first = 0
         for last in GROUP_ENDS:
             for stage, work in enumerate((totals, take_root, negate_and_store)):
-                due.setdefault(QUARTERS * last + (4 if last < GROUPS else 0) + stage, []).append((work, slice(first, last)))
+                due.setdefault(QUARTERS * last + (3 if last < GROUPS else 0) + stage, []).append((work, slice(first, last)))
             first = last
 
         order = (
@@ -408,36 +422,37 @@ def label_distances(tc, ident, emb_t, lab_t, out):
         )
         for item in clip_list[0:8]:
             clip(*item)
-        minima(minima_list[0:4])
+        minima_by_vector(minima_list[0:4])
+        minima_by_gpsimd(minima_list[0:4])
         for s in range(QUARTERS * GROUPS):
             clips = clip_list[8 + 6 * s : 14 + 6 * s]
+            now = minima_list[4 + 2 * s : 6 + 2 * s]
             for item in clips[0:2]:
                 clip(*item)
-            if s % 2 == 1 and s >= QUARTERS:
-                sum_bank(s // QUARTERS - 1, s % QUARTERS // 2)
             for work, groups in due.get(s, []):
                 work(groups)
-            for item in clips[2:]:
+            for item in clips[2:5]:
                 clip(*item)
-            now = minima_list[4 + 2 * s : 6 + 2 * s]
             if now:
-                minima(now)
-            pairs = minima_list[0:4] if s == 0 else minima_list[2 + 2 * s : 4 + 2 * s]
-            pairs = list(pairs)
+                minima_by_vector(now)
+                minima_by_gpsimd(now)
+            for item in clips[5:]:
+                clip(*item)
+            pairs = list(minima_list[0:4] if s == 0 else minima_list[2 + 2 * s : 4 + 2 * s])
             n, k = (s - 3) // 4, (s - 3) % 4
-            tiles = [(n, 2 * k), (n, 2 * k + 1)] if n >= 0 else []
+            tiles = [2 * k, 2 * k + 1] if n >= 0 else []
             if s == QUARTERS * GROUPS - 1:
-                tiles = [(n, t) for t in range(B_TILES)]
+                tiles = list(range(B_TILES))
             for i, (which, tile) in enumerate(order[s % 2]):
                 if i in (2, 6) or (s == 0 and i in (4, 8)):
                     if pairs:
                         square(*pairs.pop(0))
+                if i in (2, 5):
+                    for t in tiles[len(tiles) // 2 * (i == 5) : len(tiles) // 2 * (1 + (i == 5))]:
+                        sum_over_chunks(n, t)
+                        if t % SET_CHUNKS == SET_CHUNKS - 1:
+                            sum_bank(n, t // SET_CHUNKS)
                 bank_work(3 * (s // 2) + which, tile)
-                if i in (6, 10):
-                    for t in tiles[len(tiles) // 2 * (i == 10) : len(tiles) // 2 * (1 + (i == 10))]:
-                        sum_over_chunks(*t)
-                        if len(tiles) > 2 and t[1] % SET_CHUNKS == SET_CHUNKS - 1:
-                            sum_bank(n, t[1] // SET_CHUNKS)
         for s in range(QUARTERS * GROUPS, QUARTERS * GROUPS + 4):
             for work, groups in due.get(s, []):
                 work(groups)

@@ -262,8 +262,8 @@ QUARTERS = 4
 def label_distances(tc, ident, emb_t, lab_t, out):
     nc = tc.nc
     with ExitStack() as ctx:
-        fixed = ctx.enter_context(tc.tile_pool(name="results", bufs=1))
         diffs = ctx.enter_context(tc.tile_pool(name="diffs", bufs=4, reuse_waits="tile"))
+        fixed = ctx.enter_context(tc.tile_pool(name="results", bufs=1))
         mins = ctx.enter_context(tc.tile_pool(name="mins", bufs=4, reuse_waits="tile"))
         squares = ctx.enter_context(tc.tile_pool(name="squares", bufs=16, reuse_waits="tile"))
         waste = ctx.enter_context(tc.tile_pool(name="waste", bufs=2))
@@ -278,9 +278,6 @@ def label_distances(tc, ident, emb_t, lab_t, out):
         total = fixed.tile([P, B_TILES, L], F32)
         scores = fixed.tile([P, B_TILES, L], F32)
         neg_lab = fixed.tile([P, D_CHUNKS, GROUPS], F32)
-        nc.vector.tensor_scalar_mul(
-            out=neg_lab[:], in0=lab_t[:].rearrange("p c (n u) -> p c n u", u=GROUP)[:, :, :, 0], scalar1=-1.0
-        )
 
         sets = [(GROUP * n + u, half) for n in range(GROUPS) for u in range(1, GROUP) for half in range(HALVES)]
         clip_list = [(q, j) for q in range(len(sets)) for j in range(SET_CHUNKS)]
@@ -302,6 +299,9 @@ def label_distances(tc, ident, emb_t, lab_t, out):
             )
 
         def share(item):
+            n, c = item
+            if n == 0 and c < 4:
+                return 0
             return B if item[1] % 2 == 0 else B // 2
 
         def minima_by_vector(items):
@@ -320,14 +320,15 @@ def label_distances(tc, ident, emb_t, lab_t, out):
             nc.vector.memset(lowest[:], LOWEST)
             for n, c in items:
                 cols = slice(0, share((n, c)))
-                nc.gpsimd.tensor_scalar(
-                    out=min_of[n, c][:, cols],
-                    in0=emb_t[:, c, cols],
-                    scalar1=lab_t[:, c, GROUP * n : GROUP * n + 1],
-                    scalar2=lowest[:],
-                    op0=ALU.min,
-                    op1=ALU.max,
-                )
+                if cols.stop:
+                    nc.gpsimd.tensor_scalar(
+                        out=min_of[n, c][:, cols],
+                        in0=emb_t[:, c, cols],
+                        scalar1=lab_t[:, c, GROUP * n : GROUP * n + 1],
+                        scalar2=lowest[:],
+                        op0=ALU.min,
+                        op1=ALU.max,
+                    )
 
         def square(n, c):
             square_of[n, c] = squares.tile([P, B], F32, name="square")
@@ -359,7 +360,7 @@ def label_distances(tc, ident, emb_t, lab_t, out):
 
         def turn(pool, q, tile):
             bank = pool.tile([P, SET_CHUNKS, P], F32, name="bank")
-            for j in range(SET_CHUNKS):
+            for j in reversed(range(SET_CHUNKS)):
                 nc.tensor.transpose(bank[:, j, :], diff_of[q][:, j, tile * P : (tile + 1) * P], ident)
             return bank
 
@@ -422,8 +423,6 @@ def label_distances(tc, ident, emb_t, lab_t, out):
         )
         for item in clip_list[0:8]:
             clip(*item)
-        minima_by_vector(minima_list[0:4])
-        minima_by_gpsimd(minima_list[0:4])
         for s in range(QUARTERS * GROUPS):
             clips = clip_list[8 + 6 * s : 14 + 6 * s]
             now = minima_list[4 + 2 * s : 6 + 2 * s]
@@ -431,6 +430,11 @@ def label_distances(tc, ident, emb_t, lab_t, out):
                 clip(*item)
             for work, groups in due.get(s, []):
                 work(groups)
+            if s == 0:
+                nc.vector.tensor_scalar_mul(
+                    out=neg_lab[:], in0=lab_t[:].rearrange("p c (n u) -> p c n u", u=GROUP)[:, :, :, 0], scalar1=-1.0
+                )
+                minima_by_vector(minima_list[0:4])
             for item in clips[2:5]:
                 clip(*item)
             if now:
@@ -444,7 +448,7 @@ def label_distances(tc, ident, emb_t, lab_t, out):
             if s == QUARTERS * GROUPS - 1:
                 tiles = list(range(B_TILES))
             for i, (which, tile) in enumerate(order[s % 2]):
-                if i in (2, 6) or (s == 0 and i in (4, 8)):
+                if i in ((4, 6, 8, 10) if s == 0 else (2, 6)):
                     if pairs:
                         square(*pairs.pop(0))
                 if i in (2, 5):

from contextlib import ExitStack

import concourse.mybir as mybir
from concourse.masks import make_identity

F32 = mybir.dt.float32
BF16 = mybir.dt.bfloat16
I32 = mybir.dt.int32
U32 = mybir.dt.uint32
U8 = mybir.dt.uint8
FP8X4 = mybir.dt.float8_e4m3fn_x4
ALU = mybir.AluOpType
ACT = mybir.ActivationFunctionType

P = 128
B = 1024
DH = 2048
K1 = 2 * DH
DO = 1024
L = 128

PACK = 4
K_PASS = P * PACK
WORDS_PASS = K_PASS // 2
N_MOVING = 512
B_TILES = B // P
D_CHUNKS = DO // P
TURNS_PER_BANK = 4
PLANES_PER_TILE = 4

FLOPS = 2 * B * K1 * DO + 2 * B * DO * DO + 4 * B * L * DO


def load_quantised_weight(nc, pool, words, scales, name):
    passes, width = words.shape[0], words.shape[2]
    together = min(passes, PLANES_PER_TILE)
    codes = pool.tile([P, passes, width], U32, name=name + "_codes", align_bytes=64)
    planes = pool.tile([P, passes // together, width], U8, name=name + "_planes", align_bytes=64)
    nc.vector.memset(planes[:].bitcast(I32), 0)
    for group in range(passes // together):
        for quadrant in range(4):
            nc.sync.dma_start(
                out=planes[32 * quadrant : 32 * quadrant + 4 * together, group, :].bitcast(I32),
                in_=scales[
                    group * together : (group + 1) * together, 4 * quadrant : 4 * quadrant + 4, :
                ].bitcast(I32),
            )
    for g in range(passes):
        nc.sync.dma_start(
            out=codes[:, g, :].bitcast(I32),
            in_=words[g].rearrange("p n t -> p (n t)").bitcast(I32),
        )
    return codes, planes


def scale_plane(planes, g, cols):
    return planes[4 * (g % PLANES_PER_TILE) : P, g // PLANES_PER_TILE, cols]


def turn_k_onto_partitions(nc, psum, ident, rows, grouped_words, scalar_helps):
    words = rows.bitcast(F32)
    for pair in range(words.shape[1] // (2 * WORDS_PASS)):
        bank = psum.tile([P, TURNS_PER_BANK, P], F32, name="turned")
        for j in range(TURNS_PER_BANK):
            g, u = 2 * pair + j // 2, j % 2
            nc.tensor.transpose(
                bank[:, j, :], words[:, WORDS_PASS * g + u : WORDS_PASS * (g + 1) : 2], ident
            )
        copy = nc.scalar.copy if (scalar_helps and pair % 2 == 1) else nc.vector.tensor_copy
        copy(
            out=grouped_words[:, 2 * pair : 2 * pair + 2, :, :],
            in_=bank[:].rearrange("p (g u) r -> p g r u", u=2),
        )


AHEAD = 2


def embed(tc, ident, emb_t, lab_t, sbj_vec, obj_vec, W1_words, W1_scales, b1, W2_words, W2_scales, b2, label_vecs):
    nc = tc.nc
    passes_1, passes_2 = K1 // K_PASS, DO // K_PASS
    with ExitStack() as ctx:
        fixed = ctx.enter_context(tc.tile_pool(name="fixed", bufs=1))
        double = ctx.enter_context(tc.tile_pool(name="double", bufs=2))
        triple = ctx.enter_context(tc.tile_pool(name="triple", bufs=AHEAD + 1))
        turned = ctx.enter_context(tc.psum_pool(name="turned", bufs=4))
        sums = ctx.enter_context(tc.psum_pool(name="sums", bufs=4))

        x_rows = [fixed.tile([P, K1], BF16, name="x_rows_%d" % i) for i in range(B_TILES)]

        def load_x(i):
            b_rows = slice(i * P, (i + 1) * P)
            nc.sync.dma_start(out=x_rows[i][:, 0:DH], in_=sbj_vec[b_rows, :])
            nc.sync.dma_start(out=x_rows[i][:, DH:K1], in_=obj_vec[b_rows, :])

        for i in range(AHEAD):
            load_x(i)
        b1_row = fixed.tile([P, DO], BF16)
        nc.vector.memset(b1_row[:], 0.0)
        nc.sync.dma_start(out=b1_row[0:1, :], in_=b1.rearrange("(o n) -> o n", o=1))
        lab_rows = fixed.tile([P, DO], BF16)
        nc.sync.dma_start(out=lab_rows[:], in_=label_vecs)
        b2_rows = fixed.tile([P, P], BF16)
        nc.vector.memset(b2_rows[:], 0.0)
        nc.sync.dma_start(out=b2_rows[0:D_CHUNKS, :], in_=b2.rearrange("(c p) -> c p", p=P))
        w1_codes, w1_planes = load_quantised_weight(nc, fixed, W1_words, W1_scales, "w1")
        for i in range(AHEAD, B_TILES):
            load_x(i)
        w2_codes, w2_planes = load_quantised_weight(nc, fixed, W2_words, W2_scales, "w2")

        x_codes, x_scales, x_grouped = {}, {}, {}

        def relu_x(i):
            for part in (slice(0, DH), slice(DH, K1)):
                nc.vector.tensor_scalar_max(out=x_rows[i][:, part], in0=x_rows[i][:, part], scalar1=0.0)

        def turn_x(i):
            x_grouped[i] = double.tile([P, passes_1, P, PACK], BF16, name="x_grouped", align_bytes=64)
            turn_k_onto_partitions(nc, turned, ident, x_rows[i][:], x_grouped[i][:].bitcast(F32), True)

        def quantise_x(i):
            x_codes[i] = triple.tile([P, passes_1, P], U32, name="x_codes", align_bytes=64)
            x_scales[i] = triple.tile([P, passes_1, P], U8, name="x_scales", align_bytes=64)
            nc.vector.quantize_mx(
                out=x_codes[i][:].rearrange("p g r -> p (g r)").bitcast(FP8X4),
                scales=x_scales[i][:].rearrange("p g r -> p (g r)"),
                in_=x_grouped[i][:].rearrange("p g r t -> p (g r t)"),
            )

        b1_all = fixed.tile([P, DO], F32)

        def spread_b1():
            ones = fixed.tile([P, P], BF16)
            nc.vector.memset(ones[:], 1.0)
            for n in range(DO // N_MOVING):
                n_cols = slice(n * N_MOVING, (n + 1) * N_MOVING)
                bank = sums.tile([P, N_MOVING], F32, name="acc")
                nc.tensor.matmul(out=bank[:], lhsT=ones[:], rhs=b1_row[:, n_cols], start=True, stop=True)
                nc.vector.tensor_copy(out=b1_all[:, n_cols], in_=bank[:])

        b2_t = fixed.tile([P, D_CHUNKS], F32)

        def turn_labels_and_b2():
            lab_f32 = fixed.tile([P, DO], F32)
            nc.vector.tensor_copy(out=lab_f32[:], in_=lab_rows[:])
            b2_f32 = fixed.tile([P, P], F32)
            nc.vector.tensor_copy(out=b2_f32[:], in_=b2_rows[:])
            for half in range(D_CHUNKS // TURNS_PER_BANK):
                bank = turned.tile([P, TURNS_PER_BANK, P], F32, name="turned")
                for j in range(TURNS_PER_BANK):
                    c = half * TURNS_PER_BANK + j
                    nc.tensor.transpose(bank[:, j, :], lab_f32[:, c * P : (c + 1) * P], ident)
                nc.vector.tensor_copy(
                    out=lab_t[:, half * TURNS_PER_BANK : (half + 1) * TURNS_PER_BANK, :], in_=bank[:]
                )
            bank = turned.tile([P, TURNS_PER_BANK, P], F32, name="turned")
            nc.tensor.transpose(bank[:, 0, :], b2_f32[:], ident)
            nc.vector.tensor_copy(out=b2_t[:], in_=bank[:, 0, 0:D_CHUNKS])

        h_rows = {}
        h_grouped = fixed.tile([P, passes_2, B, PACK], BF16, align_bytes=64)
        h_codes = fixed.tile([P, passes_2, B], U32, align_bytes=64)
        h_scales = fixed.tile([P, passes_2, B], U8, align_bytes=64)

        def first_layer(i):
            halves = range(DO // N_MOVING)
            acc = [sums.tile([P, N_MOVING], F32, name="acc") for n in halves]
            for g in range(passes_1):
                for n in halves:
                    n_cols = slice(n * N_MOVING, (n + 1) * N_MOVING)
                    nc.tensor.matmul_mx(
                        out=acc[n][:],
                        lhsT=x_codes[i][:, g, :].bitcast(FP8X4),
                        lhsT_scale=x_scales[i][:, g, :],
                        rhs=w1_codes[:, g, n_cols].bitcast(FP8X4),
                        rhs_scale=scale_plane(w1_planes, g, n_cols),
                        start=(g == 0),
                        stop=(g == passes_1 - 1),
                    )
            h_rows[i] = double.tile([P, DO], BF16, name="h_rows")
            for n in halves:
                n_cols = slice(n * N_MOVING, (n + 1) * N_MOVING)
                hidden = double.tile([P, N_MOVING], F32, name="hidden")
                nc.vector.tensor_tensor(out=hidden[:], in0=acc[n][:], in1=b1_all[:, n_cols], op=ALU.add)
                nc.scalar.activation(out=h_rows[i][:, n_cols], in_=hidden[:], func=ACT.Relu)

        def turn_hidden(i):
            b_rows = slice(i * P, (i + 1) * P)
            turn_k_onto_partitions(
                nc, turned, ident, h_rows[i][:], h_grouped[:, :, b_rows, :].bitcast(F32), False
            )

        def quantise_hidden(n):
            b_cols = slice(n * N_MOVING, (n + 1) * N_MOVING)
            for g in range(passes_2):
                nc.vector.quantize_mx(
                    out=h_codes[:, g, b_cols].bitcast(FP8X4),
                    scales=h_scales[:, g, b_cols],
                    in_=h_grouped[:, g, b_cols, :].rearrange("p r t -> p (r t)"),
                )

        def second_layer(n, chunks):
            b_cols = slice(n * N_MOVING, (n + 1) * N_MOVING)
            for c in chunks:
                d_cols = slice(c * P, (c + 1) * P)
                acc = sums.tile([P, N_MOVING], F32, name="acc")
                for g in range(passes_2):
                    nc.tensor.matmul_mx(
                        out=acc[:],
                        lhsT=w2_codes[:, g, d_cols].bitcast(FP8X4),
                        lhsT_scale=scale_plane(w2_planes, g, d_cols),
                        rhs=h_codes[:, g, b_cols].bitcast(FP8X4),
                        rhs_scale=h_scales[:, g, b_cols],
                        start=(g == 0),
                        stop=(g == passes_2 - 1),
                    )
                nc.scalar.activation(
                    out=emb_t[:, c, b_cols], in_=acc[:], func=ACT.Identity, bias=b2_t[:, c : c + 1]
                )

        for i in range(AHEAD):
            relu_x(i)
            turn_x(i)
        quantise_x(0)
        turn_labels_and_b2()
        spread_b1()
        for i in range(1, AHEAD):
            quantise_x(i)
        for i in range(B_TILES):
            later = i + AHEAD
            if later < B_TILES:
                relu_x(later)
            first_layer(i)
            if i > 0:
                turn_hidden(i - 1)
                if i * P % N_MOVING == 0:
                    quantise_hidden(i * P // N_MOVING - 1)
            if later < B_TILES:
                turn_x(later)
                quantise_x(later)
        second_layer(0, range(0, D_CHUNKS // 2))
        turn_hidden(B_TILES - 1)
        second_layer(0, range(D_CHUNKS // 2, D_CHUNKS))
        quantise_hidden(B // N_MOVING - 1)
        second_layer(1, range(D_CHUNKS))


SET_CHUNKS = TURNS_PER_BANK
HALVES = D_CHUNKS // SET_CHUNKS
GROUP = 4
OTHERS = GROUP - 1
GROUPS = L // GROUP
S_TILES = 5
V_TILES = B_TILES - S_TILES
STATS = 6
GROUP_ENDS = (8, 16, 24, 30, 32)
LOWEST = -3.4028234663852886e38
SQRT_FLOOR = 1e-30
QUARTERS = 4


def label_distances(tc, ident, emb_t, lab_t, out):
    nc = tc.nc
    with ExitStack() as ctx:
        diffs = ctx.enter_context(tc.tile_pool(name="diffs", bufs=4, reuse_waits="tile"))
        fixed = ctx.enter_context(tc.tile_pool(name="results", bufs=1))
        mins = ctx.enter_context(tc.tile_pool(name="mins", bufs=4, reuse_waits="tile"))
        squares = ctx.enter_context(tc.tile_pool(name="squares", bufs=16, reuse_waits="tile"))
        waste = ctx.enter_context(tc.tile_pool(name="waste", bufs=2))
        floors = ctx.enter_context(tc.tile_pool(name="floors", bufs=2))
        banks_s = ctx.enter_context(tc.psum_pool(name="banks_s", bufs=4, reuse_waits="tile"))
        banks_v = ctx.enter_context(tc.psum_pool(name="banks_v", bufs=3, reuse_waits="tile"))
        banks_q = ctx.enter_context(tc.psum_pool(name="banks_q", bufs=1, reuse_waits="tile"))

        usum = fixed.tile([P, HALVES, B_TILES, OTHERS * GROUPS], F32)
        stats = fixed.tile([P, HALVES * V_TILES, OTHERS * GROUPS, STATS], F32)
        parts = fixed.tile([P, HALVES * V_TILES, OTHERS * GROUPS, 2], F32)
        total = fixed.tile([P, B_TILES, L], F32)
        scores = fixed.tile([P, B_TILES, L], F32)
        neg_lab = fixed.tile([P, D_CHUNKS, GROUPS], F32)

        sets = [(GROUP * n + u, half) for n in range(GROUPS) for u in range(1, GROUP) for half in range(HALVES)]
        clip_list = [(q, j) for q in range(len(sets)) for j in range(SET_CHUNKS)]
        minima_list = [(n, c) for n in range(GROUPS) for c in range(D_CHUNKS)]
        diff_of, min_of, square_of, acc_of = {}, {}, {}, {}

        def clip(q, j):
            label, half = sets[q]
            if q not in diff_of:
                diff_of[q] = diffs.tile([P, SET_CHUNKS, B], F32, name="diff")
            c = half * SET_CHUNKS + j
            nc.vector.tensor_scalar(
                out=diff_of[q][:, j, :],
                in0=emb_t[:, c, :],
                scalar1=lab_t[:, c, label : label + 1],
                scalar2=0.0,
                op0=ALU.subtract,
                op1=ALU.min,
            )

        def share(item):
            n, c = item
            if n == 0 and c < 4:
                return 0
            return B if item[1] % 2 == 0 else B // 2

        def minima_by_vector(items):
            for n, c in items:
                min_of[n, c] = mins.tile([P, B], F32, name="minimum")
                cols = slice(share((n, c)), B)
                if cols.start < B:
                    nc.vector.tensor_scalar_min(
                        out=min_of[n, c][:, cols],
                        in0=emb_t[:, c, cols],
                        scalar1=lab_t[:, c, GROUP * n : GROUP * n + 1],
                    )

        def minima_by_gpsimd(items):
            lowest = floors.tile([P, 1], F32, name="lowest")
            nc.vector.memset(lowest[:], LOWEST)
            for n, c in items:
                cols = slice(0, share((n, c)))
                if cols.stop:
                    nc.gpsimd.tensor_scalar(
                        out=min_of[n, c][:, cols],
                        in0=emb_t[:, c, cols],
                        scalar1=lab_t[:, c, GROUP * n : GROUP * n + 1],
                        scalar2=lowest[:],
                        op0=ALU.min,
                        op1=ALU.max,
                    )

        def square(n, c):
            square_of[n, c] = squares.tile([P, B], F32, name="square")
            nc.scalar.activation(
                out=square_of[n, c][:], in_=min_of[n, c][:], func=ACT.Square, bias=neg_lab[:, c, n : n + 1]
            )

        def sum_over_chunks(n, tile):
            bank = tile // SET_CHUNKS
            if (n, bank) not in acc_of:
                acc_of[n, bank] = banks_q.tile([P, SET_CHUNKS, P], F32, name="acc_q")
            for c in range(D_CHUNKS):
                nc.tensor.matmul(
                    out=acc_of[n, bank][:, tile % SET_CHUNKS, :],
                    lhsT=square_of[n, c][:, tile * P : (tile + 1) * P],
                    rhs=ident,
                    is_transpose=True,
                    start=(c == 0),
                    stop=(c == D_CHUNKS - 1),
                )

        def sum_bank(n, bank):
            nc.vector.tensor_reduce(
                out=total[:, bank * SET_CHUNKS : (bank + 1) * SET_CHUNKS, GROUP * n : GROUP * n + 1],
                in_=acc_of[n, bank][:],
                axis=mybir.AxisListType.X,
                op=ALU.add,
            )

        def turn(pool, q, tile):
            bank = pool.tile([P, SET_CHUNKS, P], F32, name="bank")
            for j in reversed(range(SET_CHUNKS)):
                nc.tensor.transpose(bank[:, j, :], diff_of[q][:, j, tile * P : (tile + 1) * P], ident)
            return bank

        def bank_work(q, tile):
            label, half = sets[q]
            place = OTHERS * (label // GROUP) + label % GROUP - 1
            if tile < S_TILES:
                bank = turn(banks_s, q, tile)
                unread = waste.tile([P, SET_CHUNKS, P], BF16, name="unread")
                nc.scalar.activation(
                    out=unread[:], in_=bank[:], func=ACT.Square, accum_out=usum[:, half, tile, place : place + 1]
                )
            else:
                bank = turn(banks_v, q, tile)
                nc.vector.bn_stats(out=stats[:, half * V_TILES + tile - S_TILES, place, :], in_=bank[:])

        def totals(groups):
            places = slice(OTHERS * groups.start, OTHERS * groups.stop)
            labels = slice(GROUP * groups.start, GROUP * groups.stop)
            triples = stats[:, :, places, :].rearrange("p q n (e s) -> p q n e s", s=3)
            mean, spread = triples[:, :, :, :, 1], triples[:, :, :, :, 2]
            some = parts[:, :, places, :]
            nc.vector.tensor_tensor(out=some, in0=mean, in1=mean, op=ALU.mult)
            nc.vector.tensor_scalar_mul(out=some, in0=some, scalar1=float(SET_CHUNKS * P // 2))
            nc.vector.tensor_tensor(out=some, in0=some, in1=spread, op=ALU.add)
            halves = some.rearrange("p (w t) n e -> p w t n e", t=V_TILES)
            nc.vector.tensor_tensor(
                out=usum[:, :, S_TILES:, places], in0=halves[:, :, :, :, 0], in1=halves[:, :, :, :, 1], op=ALU.add
            )
            nc.vector.tensor_tensor(
                out=total[:, :, labels].rearrange("p t (n u) -> p t n u", u=GROUP)[:, :, :, 1:],
                in0=usum[:, 0, :, places].rearrange("p t (n u) -> p t n u", u=OTHERS),
                in1=usum[:, 1, :, places].rearrange("p t (n u) -> p t n u", u=OTHERS),
                op=ALU.add,
            )

        def take_root(groups):
            labels = slice(GROUP * groups.start, GROUP * groups.stop)
            nc.scalar.activation(
                out=scores[:, :, labels], in_=total[:, :, labels], func=ACT.Sqrt, bias=SQRT_FLOOR
            )

        def negate_and_store(groups):
            labels = slice(GROUP * groups.start, GROUP * groups.stop)
            nc.vector.tensor_scalar_mul(out=scores[:, :, labels], in0=scores[:, :, labels], scalar1=-1.0)
            nc.sync.dma_start(
                out=out.rearrange("(t p) l -> p t l", p=P)[:, :, labels], in_=scores[:, :, labels]
            )

        due = {}
        first = 0
        for last in GROUP_ENDS:
            for stage, work in enumerate((totals, take_root, negate_and_store)):
                due.setdefault(QUARTERS * last + (3 if last < GROUPS else 0) + stage, []).append((work, slice(first, last)))
            first = last

        order = (
            [(0, t) for t in (0, 1, 5, 2, 3, 6, 4, 7)] + [(1, t) for t in (0, 5, 1, 6)],
            [(1, t) for t in (2, 3, 7, 4)] + [(2, t) for t in (0, 5, 1, 6, 2, 7, 3, 4)],
        )
        for item in clip_list[0:8]:
            clip(*item)
        for s in range(QUARTERS * GROUPS):
            clips = clip_list[8 + 6 * s : 14 + 6 * s]
            now = minima_list[4 + 2 * s : 6 + 2 * s]
            for item in clips[0:2]:
                clip(*item)
            for work, groups in due.get(s, []):
                work(groups)
            if s == 0:
                nc.vector.tensor_scalar_mul(
                    out=neg_lab[:], in0=lab_t[:].rearrange("p c (n u) -> p c n u", u=GROUP)[:, :, :, 0], scalar1=-1.0
                )
                minima_by_vector(minima_list[0:4])
            for item in clips[2:5]:
                clip(*item)
            if now:
                minima_by_vector(now)
                minima_by_gpsimd(now)
            for item in clips[5:]:
                clip(*item)
            pairs = list(minima_list[0:4] if s == 0 else minima_list[2 + 2 * s : 4 + 2 * s])
            n, k = (s - 3) // 4, (s - 3) % 4
            tiles = [2 * k, 2 * k + 1] if n >= 0 else []
            if s == QUARTERS * GROUPS - 1:
                tiles = list(range(B_TILES))
            for i, (which, tile) in enumerate(order[s % 2]):
                if i in ((4, 6, 8, 10) if s == 0 else (2, 6)):
                    if pairs:
                        square(*pairs.pop(0))
                if i in (2, 5):
                    for t in tiles[len(tiles) // 2 * (i == 5) : len(tiles) // 2 * (1 + (i == 5))]:
                        sum_over_chunks(n, t)
                        if t % SET_CHUNKS == SET_CHUNKS - 1:
                            sum_bank(n, t // SET_CHUNKS)
                bank_work(3 * (s // 2) + which, tile)
        for s in range(QUARTERS * GROUPS, QUARTERS * GROUPS + 4):
            for work, groups in due.get(s, []):
                work(groups)


def tile_relationembedding_kernel(
    tc, sbj_vec, obj_vec, W1_words, W1_scales, b1, W2_words, W2_scales, b2, label_vecs, out
):
    nc = tc.nc
    with tc.manual_schedule(), tc.tile_pool(name="keep", bufs=1) as keep:
        ident = keep.tile([P, P], F32)
        make_identity(nc, ident[:])
        one = keep.tile([P, 1], F32)
        nc.vector.memset(one[:], 1.0)
        nc.scalar.activation(out=one[:], in_=one[:], func=ACT.Sqrt)
        emb_t = keep.tile([P, D_CHUNKS, B], F32)
        lab_t = keep.tile([P, D_CHUNKS, L], F32)
        embed(
            tc, ident[:], emb_t, lab_t,
            sbj_vec, obj_vec, W1_words, W1_scales, b1, W2_words, W2_scales, b2, label_vecs,
        )
        label_distances(tc, ident[:], emb_t, lab_t, out)
